import numpy as np
import ml_dtypes


def mxq(x, axis, fmt="e4m3"):
    dtype, down = {"e4m3": (ml_dtypes.float8_e4m3fn, 7), "e5m2": (ml_dtypes.float8_e5m2, 14)}[fmt]
    v = np.moveaxis(np.asarray(x, np.float32).astype(ml_dtypes.bfloat16).astype(np.float64), axis, -1)
    blocks = v.reshape(v.shape[:-1] + (-1, 32))
    amax = np.abs(blocks).max(-1, keepdims=True)
    byte = np.maximum(np.where(amax > 0, np.frexp(amax)[1] - 1 + 127, 0) - down, 1)
    scale = np.exp2(byte - 127.0)
    codes = (blocks / scale).astype(np.float32).astype(dtype).astype(np.float64)
    return np.moveaxis((codes * scale).reshape(v.shape), -1, axis)


WIDE = False


def mx_kscale(k):
    if not WIDE:
        return np.ones(k)
    levels = np.array([10, -10, 5, -5, 0])
    a = np.random.permutation(np.resize(levels, k // 512 * 4)).reshape(k // 512, 4)
    idx = np.arange(k)
    return np.exp2(a[idx // 512, idx % 128 // 32])


BF16 = ml_dtypes.bfloat16


def bf(x):
    return np.asarray(x, np.float32).astype(BF16)


def f64(x):
    return np.asarray(x).astype(np.float64)


B, I, H, AH, AI, G = 512, 1024, 1024, 128, 128, 4
EPS = 1e-5
K = I + H


def sigmoid(v):
    return 1.0 / (1.0 + np.exp(-v))


def ln(v, w, b):
    mu = v.mean(-1, keepdims=True)
    var = ((v - mu) ** 2).mean(-1, keepdims=True)
    return (v - mu) / np.sqrt(var + EPS) * w + b


def setup_inputs():
    n = np.random.standard_normal
    s = mx_kscale(K)
    return {
        "x": bf(n((B, I)) * s[:I]),
        "hx": bf(n((B, H)) * s[I:]),
        "ah": bf(n((B, AH))),
        "ac": bf(n((B, AH))),
        "a_w_ih": bf(n((G * AH, K)) / np.sqrt(K) / s),
        "a_w_hh": bf(n((G * AH, AH)) / np.sqrt(AH)),
        "a_ln_i_w": bf(1.0 + 0.1 * n(G * AH)),
        "a_ln_i_b": bf(0.2 * n(G * AH)),
        "a_ln_h_w": bf(1.0 + 0.1 * n(G * AH)),
        "a_ln_h_b": bf(0.2 * n(G * AH)),
        "a_ln_c_w": bf(1.0 + 0.1 * n(AH)),
        "a_ln_c_b": bf(0.2 * n(AH)),
    }


def reference(x, hx, ah, ac, a_w_ih, a_w_hh, a_ln_i_w, a_ln_i_b, a_ln_h_w, a_ln_h_b, a_ln_c_w, a_ln_c_b):
    ai = np.concatenate([f64(x), f64(hx)], axis=1)
    ig = ln(mxq(ai, 1, "e4m3") @ mxq(f64(a_w_ih), 1, "e4m3").T, f64(a_ln_i_w), f64(a_ln_i_b))
    hg = ln(f64(ah) @ f64(a_w_hh).T, f64(a_ln_h_w), f64(a_ln_h_b))
    g = ig + hg
    gi, gf, gj, go = np.split(g, G, axis=1)
    acy = ln(sigmoid(gf) * f64(ac) + sigmoid(gi) * np.tanh(gj), f64(a_ln_c_w), f64(a_ln_c_b))
    ada = sigmoid(go) * np.tanh(acy)
    return ada, acy

@@ -1,0 +1,287 @@
+from contextlib import ExitStack
+
+import concourse.mybir as mybir
+from concourse.masks import make_identity
+
+F32 = mybir.dt.float32
+BF16 = mybir.dt.bfloat16
+U32 = mybir.dt.uint32
+U8 = mybir.dt.uint8
+FP8X4 = mybir.dt.float8_e4m3fn_x4
+ALU = mybir.AluOpType
+ACT = mybir.ActivationFunctionType
+
+P = 128
+B, I, H, AH, G = 512, 1024, 1024, 128, 4
+K = I + H
+N = G * AH
+NT = B // P
+NG = K // 512
+EPS = 1e-5
+FLOPS = 2 * B * K * N + 2 * B * AH * N
+
+
+def tile_adaptivelstmcell_pa_kernel(
+    tc, x, hx, ah, ac, a_w_ih, a_w_hh, a_ln_i_w, a_ln_i_b, a_ln_h_w, a_ln_h_b, a_ln_c_w, a_ln_c_b, out_0, out_1
+):
+    nc = tc.nc
+    with ExitStack() as ctx:
+        sb = ctx.enter_context(tc.tile_pool(name="sb", bufs=1))
+        tp = ctx.enter_context(tc.psum_pool(name="tp", bufs=4))
+        acc = ctx.enter_context(tc.psum_pool(name="acc", bufs=4))
+        ctx.enter_context(tc.manual_schedule())
+
+        def per_tile(shape, dtype, name, align=None):
+            return [sb.tile(shape, dtype, name="%s%d" % (name, t), align_bytes=align) for t in range(NT)]
+
+        vrows = sb.tile([P, P], BF16)
+        nc.vector.memset(vrows[:], 0.0)
+        warm = sb.tile([P, 1], F32)
+        nc.vector.memset(warm[:], 0.0)
+        neghalf = sb.tile([P, NT], F32)
+        nc.vector.memset(neghalf[:], -0.5)
+        ident_b = sb.tile([P, P], BF16)
+        make_identity(nc, ident_b[:])
+        ident_f = sb.tile([P, P], F32)
+        make_identity(nc, ident_f[:])
+
+        ah_sb = sb.tile([P, NT * AH], BF16)
+        nc.sync.dma_start(out=ah_sb[:], in_=ah.rearrange("(p t) k -> p (t k)", t=NT))
+        whh_sb = sb.tile([P, G, AH], BF16)
+        nc.sync.dma_start(out=whh_sb[:], in_=a_w_hh.rearrange("(j p) k -> p j k", p=P))
+        for i, vec in enumerate((a_ln_i_w, a_ln_i_b, a_ln_h_w, a_ln_h_b)):
+            nc.scalar.dma_start(out=vrows[4 * i : 4 * i + 4, :], in_=vec.rearrange("(r c) -> r c", c=P))
+        warm2 = sb.tile([P, 1], F32)
+        nc.scalar.activation(out=warm2[:], in_=warm[:], func=ACT.Sigmoid)
+        w_sb = per_tile([P, K], BF16, "w_sb")
+        for j in range(G):
+            nc.sync.dma_start(out=w_sb[j][:], in_=a_w_ih[j * P : (j + 1) * P, :])
+        a_sb = per_tile([P, K], BF16, "a_sb")
+        x_v = x.rearrange("(p t) k -> p t k", t=NT)
+        hx_v = hx.rearrange("(p t) k -> p t k", t=NT)
+        for t in range(NT):
+            nc.sync.dma_start(out=a_sb[t][:, 0:I], in_=x_v[:, t, :])
+            nc.sync.dma_start(out=a_sb[t][:, I:K], in_=hx_v[:, t, :])
+        ac_sb = sb.tile([P, NT * AH], BF16)
+        nc.sync.dma_start(out=ac_sb[:], in_=ac.rearrange("(p t) c -> p (t c)", t=NT))
+        wc_sb = sb.tile([P, AH], BF16)
+        nc.sync.dma_start(out=wc_sb[:], in_=a_ln_c_w.partition_broadcast(P))
+        bc_sb = sb.tile([P, AH], BF16)
+        nc.sync.dma_start(out=bc_sb[:], in_=a_ln_c_b.partition_broadcast(P))
+
+        ahT = sb.tile([P, NT * P], BF16)
+        whhT = sb.tile([P, N], BF16)
+        vcol = sb.tile([P, 16], F32)
+        bsum = sb.tile([P, 4], F32)
+        gains = [sb.tile([P, N], F32, name="gain%d" % i) for i in range(3)]
+        Wh, Bs, Wi = gains
+        wgrp = sb.tile([P, NG * N * 4], BF16, align_bytes=64)
+        wgrp_f = wgrp[:].bitcast(F32).rearrange("p (g j r u) -> p g j r u", g=NG, j=G, u=2)
+        w_codes = sb.tile([P, NG * N], U32, align_bytes=64)
+        w_scales = sb.tile([P, NG * N], U8, align_bytes=64)
+        agrp = per_tile([P, NG * P * 4], BF16, "agrp", 64)
+        a_codes = per_tile([P, NG * P], U32, "a_codes", 64)
+        a_scales = per_tile([P, NG * P], U8, "a_scales", 64)
+        st_h = per_tile([P, 6], F32, "st_h")
+        mv_h = sb.tile([P, NT, 2], F32)
+        ve_h = sb.tile([P, NT], F32)
+        rs_h = sb.tile([P, NT], F32)
+        a_h = per_tile([P, N], F32, "a_h")
+        h_t = per_tile([P, N], F32, "h_t")
+        v_i = per_tile([P, N], F32, "v_i")
+        junk = sb.tile([P, N], BF16)
+        sum_i = per_tile([P, 1], F32, "sum_i")
+        nm_i = per_tile([P, 1], F32, "nm_i")
+        ssq_i = per_tile([P, 1], F32, "ssq_i")
+        ve_i = per_tile([P, 1], F32, "ve_i")
+        rs_i = per_tile([P, 1], F32, "rs_i")
+        a_i = per_tile([P, N], F32, "a_i")
+        gt = per_tile([P, N], F32, "gt")
+        sg = per_tile([P, N], F32, "sg")
+        m1 = per_tile([P, AH], F32, "m1")
+        m2 = per_tile([P, AH], F32, "m2")
+        cc = per_tile([P, AH], F32, "cc")
+        st_c = per_tile([P, 6], F32, "st_c")
+        mv_c = per_tile([P, 2], F32, "mv_c")
+        ve_c = per_tile([P, 1], F32, "ve_c")
+        rs_c = per_tile([P, 1], F32, "rs_c")
+        a_c = per_tile([P, AH], F32, "a_c")
+        acy = per_tile([P, AH], F32, "acy")
+        th = per_tile([P, AH], F32, "th")
+        ada = per_tile([P, AH], F32, "ada")
+        hg_ps = {}
+        ig_ps = {}
+        a_ps = {}
+        o0_v = out_0.rearrange("(p t) c -> p t c", t=NT)
+        o1_v = out_1.rearrange("(p t) c -> p t c", t=NT)
+
+        def transposed_bank(src, h):
+            src_f = src[:].bitcast(F32)
+            ps = tp.tile([P, 4 * P], F32, name="ps_t", tag="tp")
+            for i in range(4):
+                c0 = 512 * h + P * i
+                nc.tensor.transpose(ps[:, i * P : (i + 1) * P], src_f[:, c0 : c0 + P], ident_f[:])
+            return ps[:].rearrange("p (g u r) -> p g r u", g=2, u=2)
+
+        def spread(cols, dst):
+            ps = tp.tile([P, N], F32, name="ps_s", tag="tp")
+            for i in range(4):
+                nc.tensor.transpose(ps[:, i * P : (i + 1) * P], cols[:, i : i + 1].to_broadcast([P, P]), ident_f[:])
+            nc.scalar.copy(out=dst[:], in_=ps[:])
+
+        def hg_centre(t):
+            nc.vector.scalar_tensor_tensor(
+                out=a_h[t][:], in0=hg_ps[t][:], scalar=mv_h[:, t, 0:1], in1=Wh[:], op0=ALU.subtract, op1=ALU.mult
+            )
+
+        def hg_scale(t):
+            nc.vector.scalar_tensor_tensor(
+                out=h_t[t][:], in0=a_h[t][:], scalar=rs_h[:, t : t + 1], in1=Bs[:], op0=ALU.mult, op1=ALU.add
+            )
+
+        def quantise(codes, scales, grouped, c0, cols):
+            nc.vector.quantize_mx(
+                out=codes[:, c0 : c0 + cols].bitcast(FP8X4),
+                scales=scales[:, c0 : c0 + cols],
+                in_=grouped[:, 4 * c0 : 4 * (c0 + cols)],
+            )
+
+        def a_transpose(t):
+            a_ps[t] = [transposed_bank(a_sb[t], h) for h in range(2)]
+
+        def a_copy(t):
+            agrp_f = agrp[t][:].bitcast(F32).rearrange("p (g r u) -> p g r u", g=NG, u=2)
+            for h in range(2):
+                nc.scalar.copy(out=agrp_f[:, 2 * h : 2 * h + 2, :, :], in_=a_ps[t][h])
+
+        def a_multiply(t):
+            for h in range(2):
+                quantise(a_codes[t], a_scales[t], agrp[t], h * 2 * P, 2 * P)
+            ig_ps[t] = acc.tile([P, N], F32, name="ig_ps", tag="acc")
+            for g in range(NG):
+                nc.tensor.matmul_mx(
+                    out=ig_ps[t][:],
+                    lhsT=a_codes[t][:, g * P : (g + 1) * P].bitcast(FP8X4),
+                    lhsT_scale=a_scales[t][:, g * P : (g + 1) * P],
+                    rhs=w_codes[:, g * N : (g + 1) * N].bitcast(FP8X4),
+                    rhs_scale=w_scales[:, g * N : (g + 1) * N],
+                    start=(g == 0),
+                    stop=(g == NG - 1),
+                )
+
+        def ig_stats(t):
+            nc.scalar.activation(out=v_i[t][:], in_=ig_ps[t][:], func=ACT.Identity, accum_out=sum_i[t][:])
+            nc.scalar.mul(out=nm_i[t][:], in_=sum_i[t][:], mul=-1.0 / N)
+            nc.scalar.activation(out=junk[:], in_=v_i[t][:], func=ACT.Square, bias=nm_i[t][:], accum_out=ssq_i[t][:])
+            nc.gpsimd.tensor_scalar(
+                out=ve_i[t][:], in0=ssq_i[t][:], scalar1=1.0 / N, scalar2=EPS, op0=ALU.mult, op1=ALU.add
+            )
+            nc.gpsimd.tensor_tensor(out=rs_i[t][:], in0=ve_i[t][:], in1=neghalf[:, 0:1], op=ALU.pow)
+
+        def ig_centre(t):
+            nc.vector.scalar_tensor_tensor(
+                out=a_i[t][:], in0=v_i[t][:], scalar=nm_i[t][:], in1=Wi[:], op0=ALU.add, op1=ALU.mult
+            )
+
+        def gates(t):
+            nc.vector.scalar_tensor_tensor(
+                out=gt[t][:], in0=a_i[t][:], scalar=rs_i[t][:], in1=h_t[t][:], op0=ALU.mult, op1=ALU.add
+            )
+            nc.scalar.activation(out=sg[t][:, 0 : 2 * AH], in_=gt[t][:, 0 : 2 * AH], func=ACT.Sigmoid)
+            nc.scalar.activation(out=sg[t][:, 2 * AH : 3 * AH], in_=gt[t][:, 2 * AH : 3 * AH], func=ACT.Tanh)
+            nc.scalar.activation(out=sg[t][:, 3 * AH : 4 * AH], in_=gt[t][:, 3 * AH : 4 * AH], func=ACT.Sigmoid)
+
+        def cell(t):
+            nc.vector.tensor_tensor(
+                out=m1[t][:], in0=sg[t][:, AH : 2 * AH], in1=ac_sb[:, t * AH : (t + 1) * AH], op=ALU.mult
+            )
+            nc.vector.tensor_tensor(out=m2[t][:], in0=sg[t][:, 0:AH], in1=sg[t][:, 2 * AH : 3 * AH], op=ALU.mult)
+            nc.vector.tensor_tensor(out=cc[t][:], in0=m1[t][:], in1=m2[t][:], op=ALU.add)
+            nc.vector.bn_stats(out=st_c[t][:], in_=cc[t][:])
+            nc.vector.bn_aggr(out=mv_c[t][:], in_=st_c[t][:])
+            nc.gpsimd.tensor_scalar(
+                out=ve_c[t][:], in0=mv_c[t][:, 1:2], scalar1=EPS, scalar2=1.0, op0=ALU.add, op1=ALU.mult
+            )
+            nc.gpsimd.tensor_tensor(out=rs_c[t][:], in0=ve_c[t][:], in1=neghalf[:, 0:1], op=ALU.pow)
+            nc.vector.scalar_tensor_tensor(
+                out=a_c[t][:], in0=cc[t][:], scalar=mv_c[t][:, 0:1], in1=wc_sb[:], op0=ALU.subtract, op1=ALU.mult
+            )
+
+        def cell_out(t):
+            nc.vector.scalar_tensor_tensor(
+                out=acy[t][:], in0=a_c[t][:], scalar=rs_c[t][:], in1=bc_sb[:], op0=ALU.mult, op1=ALU.add
+            )
+            nc.sync.dma_start(out=o1_v[:, t, :], in_=acy[t][:])
+            nc.scalar.activation(out=th[t][:], in_=acy[t][:], func=ACT.Tanh)
+
+        def hidden_out(t):
+            nc.vector.tensor_tensor(out=ada[t][:], in0=sg[t][:, 3 * AH : 4 * AH], in1=th[t][:], op=ALU.mult)
+            nc.sync.dma_start(out=o0_v[:, t, :], in_=ada[t][:])
+
+        ahT_ps = tp.tile([P, NT * P], BF16, tag="tp")
+        for t in range(NT):
+            nc.tensor.transpose(ahT_ps[:, t * P : (t + 1) * P], ah_sb[:, t * AH : (t + 1) * AH], ident_b[:])
+        nc.vector.tensor_copy(out=ahT[:], in_=ahT_ps[:])
+        whhT_ps = tp.tile([P, N], BF16, tag="tp")
+        for j in range(G):
+            nc.tensor.transpose(whhT_ps[:, j * P : (j + 1) * P], whh_sb[:, j, :], ident_b[:])
+        nc.scalar.copy(out=whhT[:], in_=whhT_ps[:])
+        vT_ps = tp.tile([P, P], BF16, tag="tp")
+        nc.tensor.transpose(vT_ps[:], vrows[:], ident_b[:])
+        nc.vector.tensor_copy(out=vcol[:], in_=vT_ps[:, 0:16])
+        nc.vector.tensor_add(out=bsum[:], in0=vcol[:, 4:8], in1=vcol[:, 12:16])
+        spread_cols = (vcol[:, 8:12], bsum[:], vcol[:, 0:4])
+
+        for j in range(G):
+            banks = [transposed_bank(w_sb[j], h) for h in range(2)]
+            for h in range(2):
+                nc.scalar.copy(out=wgrp_f[:, 2 * h : 2 * h + 2, j, :, :], in_=banks[h])
+            if j == 0:
+                for t in range(NT):
+                    hg_ps[t] = acc.tile([P, N], F32, name="hg_ps", tag="acc")
+                    nc.tensor.matmul(hg_ps[t][:], lhsT=ahT[:, t * P : (t + 1) * P], rhs=whhT[:], start=True, stop=True)
+            if j < 3:
+                spread(spread_cols[j], gains[j])
+            if j == 0:
+                for t in range(NT):
+                    nc.vector.bn_stats(out=st_h[t][:], in_=hg_ps[t][:])
+                    nc.vector.bn_aggr(out=mv_h[:, t, :], in_=st_h[t][:])
+                nc.gpsimd.tensor_scalar(
+                    out=ve_h[:], in0=mv_h[:, :, 1], scalar1=EPS, scalar2=1.0, op0=ALU.add, op1=ALU.mult
+                )
+                nc.gpsimd.tensor_tensor(out=rs_h[:], in0=ve_h[:], in1=neghalf[:], op=ALU.pow)
+            if j == 1:
+                hg_centre(0)
+                hg_centre(1)
+            if j == 2:
+                hg_scale(0)
+                hg_scale(1)
+            if j % 2 == 1:
+                for g in range(NG):
+                    quantise(w_codes, w_scales, wgrp, g * N + (j - 1) * P, 2 * P)
+
+        def live(t):
+            return 0 <= t < NT
+
+        for r in range(-4, NT + 4):
+            if live(r):
+                ig_stats(r)
+            if live(r + 4):
+                a_transpose(r + 4)
+            if live(r + 3):
+                a_copy(r + 3)
+            if r in (-2, -1):
+                hg_centre(r + 4)
+                hg_scale(r + 4)
+            if live(r + 2):
+                a_multiply(r + 2)
+            if live(r - 2):
+                cell(r - 2)
+            if live(r - 1):
+                gates(r - 1)
+            if live(r - 3):
+                cell_out(r - 3)
+            if live(r):
+                ig_centre(r)
+            if live(r - 4):
+                hidden_out(r - 4)

@@ -34,8 +34,10 @@ def tile_adaptivelstmcell_pa_kernel(
         def per_tile(shape, dtype, name, align=None):
             return [sb.tile(shape, dtype, name="%s%d" % (name, t), align_bytes=align) for t in range(NT)]
 
-        vrows = sb.tile([P, P], BF16)
-        nc.vector.memset(vrows[:], 0.0)
+        rows = sb.tile([P, 2 * N], BF16)
+        nc.vector.memset(rows[:], 0.0)
+        ones = sb.tile([P, P], BF16)
+        nc.vector.memset(ones[:], 1.0)
         warm = sb.tile([P, 1], F32)
         nc.vector.memset(warm[:], 0.0)
         neghalf = sb.tile([P, NT], F32)
@@ -45,12 +47,16 @@ def tile_adaptivelstmcell_pa_kernel(
         ident_f = sb.tile([P, P], F32)
         make_identity(nc, ident_f[:])
 
+        def as_row(vec):
+            return vec.rearrange("(o n) -> o n", o=1)
+
         ah_sb = sb.tile([P, NT * AH], BF16)
         nc.sync.dma_start(out=ah_sb[:], in_=ah.rearrange("(p t) k -> p (t k)", t=NT))
         whh_sb = sb.tile([P, G, AH], BF16)
         nc.sync.dma_start(out=whh_sb[:], in_=a_w_hh.rearrange("(j p) k -> p j k", p=P))
-        for i, vec in enumerate((a_ln_i_w, a_ln_i_b, a_ln_h_w, a_ln_h_b)):
-            nc.scalar.dma_start(out=vrows[4 * i : 4 * i + 4, :], in_=vec.rearrange("(r c) -> r c", c=P))
+        nc.scalar.dma_start(out=rows[0:1, 0:N], in_=as_row(a_ln_h_w))
+        nc.scalar.dma_start(out=rows[0:1, N : 2 * N], in_=as_row(a_ln_i_b))
+        nc.scalar.dma_start(out=rows[1:2, N : 2 * N], in_=as_row(a_ln_h_b))
         warm2 = sb.tile([P, 1], F32)
         nc.scalar.activation(out=warm2[:], in_=warm[:], func=ACT.Sigmoid)
         w_sb = per_tile([P, K], BF16, "w_sb")
@@ -62,19 +68,19 @@ def tile_adaptivelstmcell_pa_kernel(
         for t in range(NT):
             nc.sync.dma_start(out=a_sb[t][:, 0:I], in_=x_v[:, t, :])
             nc.sync.dma_start(out=a_sb[t][:, I:K], in_=hx_v[:, t, :])
-        ac_sb = sb.tile([P, NT * AH], BF16)
-        nc.sync.dma_start(out=ac_sb[:], in_=ac.rearrange("(p t) c -> p (t c)", t=NT))
-        wc_sb = sb.tile([P, AH], BF16)
-        nc.sync.dma_start(out=wc_sb[:], in_=a_ln_c_w.partition_broadcast(P))
-        bc_sb = sb.tile([P, AH], BF16)
-        nc.sync.dma_start(out=bc_sb[:], in_=a_ln_c_b.partition_broadcast(P))
+        ac_sb = sb.tile([P, NT, AH], BF16)
+        nc.sync.dma_start(out=ac_sb[:], in_=ac.rearrange("(p t) c -> p t c", t=NT))
+        Wi = sb.tile([P, N], BF16)
+        nc.sync.dma_start(out=Wi[:], in_=a_ln_i_w.partition_broadcast(P))
+        Wc = sb.tile([P, AH], BF16)
+        nc.sync.dma_start(out=Wc[:], in_=a_ln_c_w.partition_broadcast(P))
+        Bc = sb.tile([P, AH], BF16)
+        nc.sync.dma_start(out=Bc[:], in_=a_ln_c_b.partition_broadcast(P))
 
         ahT = sb.tile([P, NT * P], BF16)
         whhT = sb.tile([P, N], BF16)
-        vcol = sb.tile([P, 16], F32)
-        bsum = sb.tile([P, 4], F32)
-        gains = [sb.tile([P, N], F32, name="gain%d" % i) for i in range(3)]
-        Wh, Bs, Wi = gains
+        Wh = sb.tile([P, N], F32)
+        Bs = sb.tile([P, N], F32)
         wgrp = sb.tile([P, NG * N * 4], BF16, align_bytes=64)
         wgrp_f = wgrp[:].bitcast(F32).rearrange("p (g j r u) -> p g j r u", g=NG, j=G, u=2)
         w_codes = sb.tile([P, NG * N], U32, align_bytes=64)
@@ -82,38 +88,53 @@ def tile_adaptivelstmcell_pa_kernel(
         agrp = per_tile([P, NG * P * 4], BF16, "agrp", 64)
         a_codes = per_tile([P, NG * P], U32, "a_codes", 64)
         a_scales = per_tile([P, NG * P], U8, "a_scales", 64)
-        st_h = per_tile([P, 6], F32, "st_h")
-        mv_h = sb.tile([P, NT, 2], F32)
-        ve_h = sb.tile([P, NT], F32)
-        rs_h = sb.tile([P, NT], F32)
         a_h = per_tile([P, N], F32, "a_h")
         h_t = per_tile([P, N], F32, "h_t")
-        v_i = per_tile([P, N], F32, "v_i")
-        junk = sb.tile([P, N], BF16)
-        sum_i = per_tile([P, 1], F32, "sum_i")
-        nm_i = per_tile([P, 1], F32, "nm_i")
-        ssq_i = per_tile([P, 1], F32, "ssq_i")
-        ve_i = per_tile([P, 1], F32, "ve_i")
-        rs_i = per_tile([P, 1], F32, "rs_i")
         a_i = per_tile([P, N], F32, "a_i")
         gt = per_tile([P, N], F32, "gt")
-        sg = per_tile([P, N], F32, "sg")
-        m1 = per_tile([P, AH], F32, "m1")
-        m2 = per_tile([P, AH], F32, "m2")
-        cc = per_tile([P, AH], F32, "cc")
-        st_c = per_tile([P, 6], F32, "st_c")
-        mv_c = per_tile([P, 2], F32, "mv_c")
-        ve_c = per_tile([P, 1], F32, "ve_c")
-        rs_c = per_tile([P, 1], F32, "rs_c")
-        a_c = per_tile([P, AH], F32, "a_c")
-        acy = per_tile([P, AH], F32, "acy")
-        th = per_tile([P, AH], F32, "th")
-        ada = per_tile([P, AH], F32, "ada")
-        hg_ps = {}
-        ig_ps = {}
-        a_ps = {}
+        sg = sb.tile([P, NT, N], F32)
+        m1 = sb.tile([P, NT, AH], F32)
+        m2 = sb.tile([P, NT, AH], F32)
+        cc = sb.tile([P, NT, AH], F32)
+        a_c = sb.tile([P, NT, AH], F32)
+        acy = sb.tile([P, NT, AH], F32)
+        th = sb.tile([P, NT, AH], F32)
+        ada = sb.tile([P, NT, AH], F32)
         o0_v = out_0.rearrange("(p t) c -> p t c", t=NT)
         o1_v = out_1.rearrange("(p t) c -> p t c", t=NT)
+
+        def norm_tiles(name):
+            st = per_tile([P, 6], F32, "st_" + name)
+            mv = sb.tile([P, NT, 2], F32, name="mv_" + name)
+            ve = sb.tile([P, NT], F32, name="ve_" + name)
+            rs = sb.tile([P, NT], F32, name="rs_" + name)
+            return st, mv, ve, rs
+
+        def mean_var(tiles, srcs):
+            st, mv, ve, rs = tiles
+            for t in range(NT):
+                nc.vector.bn_stats(out=st[t][:], in_=srcs[t])
+            for t in range(NT):
+                nc.vector.bn_aggr(out=mv[:, t, :], in_=st[t][:])
+
+        def rstd(tiles, t0, t1):
+            st, mv, ve, rs = tiles
+            nc.vector.tensor_scalar_add(out=ve[:, t0:t1], in0=mv[:, t0:t1, 1], scalar1=EPS)
+            nc.gpsimd.tensor_tensor(out=rs[:, t0:t1], in0=ve[:, t0:t1], in1=neghalf[:, t0:t1], op=ALU.pow)
+
+        def centre_gain(out, src, tiles, t, gain):
+            nc.vector.scalar_tensor_tensor(
+                out=out, in0=src, scalar=tiles[1][:, t, 0:1], in1=gain, op0=ALU.subtract, op1=ALU.mult
+            )
+
+        def scale_shift(out, src, tiles, t, shift):
+            nc.vector.scalar_tensor_tensor(
+                out=out, in0=src, scalar=tiles[3][:, t : t + 1], in1=shift, op0=ALU.mult, op1=ALU.add
+            )
+
+        ln_h = norm_tiles("h")
+        ln_i = norm_tiles("i")
+        ln_c = norm_tiles("c")
 
         def transposed_bank(src, h):
             src_f = src[:].bitcast(F32)
@@ -123,22 +144,6 @@ def tile_adaptivelstmcell_pa_kernel(
                 nc.tensor.transpose(ps[:, i * P : (i + 1) * P], src_f[:, c0 : c0 + P], ident_f[:])
             return ps[:].rearrange("p (g u r) -> p g r u", g=2, u=2)
 
-        def spread(cols, dst):
-            ps = tp.tile([P, N], F32, name="ps_s", tag="tp")
-            for i in range(4):
-                nc.tensor.transpose(ps[:, i * P : (i + 1) * P], cols[:, i : i + 1].to_broadcast([P, P]), ident_f[:])
-            nc.scalar.copy(out=dst[:], in_=ps[:])
-
-        def hg_centre(t):
-            nc.vector.scalar_tensor_tensor(
-                out=a_h[t][:], in0=hg_ps[t][:], scalar=mv_h[:, t, 0:1], in1=Wh[:], op0=ALU.subtract, op1=ALU.mult
-            )
-
-        def hg_scale(t):
-            nc.vector.scalar_tensor_tensor(
-                out=h_t[t][:], in0=a_h[t][:], scalar=rs_h[:, t : t + 1], in1=Bs[:], op0=ALU.mult, op1=ALU.add
-            )
-
         def quantise(codes, scales, grouped, c0, cols):
             nc.vector.quantize_mx(
                 out=codes[:, c0 : c0 + cols].bitcast(FP8X4),
@@ -146,142 +151,89 @@ def tile_adaptivelstmcell_pa_kernel(
                 in_=grouped[:, 4 * c0 : 4 * (c0 + cols)],
             )
 
-        def a_transpose(t):
-            a_ps[t] = [transposed_bank(a_sb[t], h) for h in range(2)]
-
-        def a_copy(t):
-            agrp_f = agrp[t][:].bitcast(F32).rearrange("p (g r u) -> p g r u", g=NG, u=2)
-            for h in range(2):
-                nc.scalar.copy(out=agrp_f[:, 2 * h : 2 * h + 2, :, :], in_=a_ps[t][h])
-
-        def a_multiply(t):
-            for h in range(2):
-                quantise(a_codes[t], a_scales[t], agrp[t], h * 2 * P, 2 * P)
-            ig_ps[t] = acc.tile([P, N], F32, name="ig_ps", tag="acc")
-            for g in range(NG):
-                nc.tensor.matmul_mx(
-                    out=ig_ps[t][:],
-                    lhsT=a_codes[t][:, g * P : (g + 1) * P].bitcast(FP8X4),
-                    lhsT_scale=a_scales[t][:, g * P : (g + 1) * P],
-                    rhs=w_codes[:, g * N : (g + 1) * N].bitcast(FP8X4),
-                    rhs_scale=w_scales[:, g * N : (g + 1) * N],
-                    start=(g == 0),
-                    stop=(g == NG - 1),
-                )
-
-        def ig_stats(t):
-            nc.scalar.activation(out=v_i[t][:], in_=ig_ps[t][:], func=ACT.Identity, accum_out=sum_i[t][:])
-            nc.scalar.mul(out=nm_i[t][:], in_=sum_i[t][:], mul=-1.0 / N)
-            nc.scalar.activation(out=junk[:], in_=v_i[t][:], func=ACT.Square, bias=nm_i[t][:], accum_out=ssq_i[t][:])
-            nc.gpsimd.tensor_scalar(
-                out=ve_i[t][:], in0=ssq_i[t][:], scalar1=1.0 / N, scalar2=EPS, op0=ALU.mult, op1=ALU.add
-            )
-            nc.gpsimd.tensor_tensor(out=rs_i[t][:], in0=ve_i[t][:], in1=neghalf[:, 0:1], op=ALU.pow)
-
-        def ig_centre(t):
-            nc.vector.scalar_tensor_tensor(
-                out=a_i[t][:], in0=v_i[t][:], scalar=nm_i[t][:], in1=Wi[:], op0=ALU.add, op1=ALU.mult
-            )
-
-        def gates(t):
-            nc.vector.scalar_tensor_tensor(
-                out=gt[t][:], in0=a_i[t][:], scalar=rs_i[t][:], in1=h_t[t][:], op0=ALU.mult, op1=ALU.add
-            )
-            nc.scalar.activation(out=sg[t][:, 0 : 2 * AH], in_=gt[t][:, 0 : 2 * AH], func=ACT.Sigmoid)
-            nc.scalar.activation(out=sg[t][:, 2 * AH : 3 * AH], in_=gt[t][:, 2 * AH : 3 * AH], func=ACT.Tanh)
-            nc.scalar.activation(out=sg[t][:, 3 * AH : 4 * AH], in_=gt[t][:, 3 * AH : 4 * AH], func=ACT.Sigmoid)
-
-        def cell(t):
-            nc.vector.tensor_tensor(
-                out=m1[t][:], in0=sg[t][:, AH : 2 * AH], in1=ac_sb[:, t * AH : (t + 1) * AH], op=ALU.mult
-            )
-            nc.vector.tensor_tensor(out=m2[t][:], in0=sg[t][:, 0:AH], in1=sg[t][:, 2 * AH : 3 * AH], op=ALU.mult)
-            nc.vector.tensor_tensor(out=cc[t][:], in0=m1[t][:], in1=m2[t][:], op=ALU.add)
-            nc.vector.bn_stats(out=st_c[t][:], in_=cc[t][:])
-            nc.vector.bn_aggr(out=mv_c[t][:], in_=st_c[t][:])
-            nc.gpsimd.tensor_scalar(
-                out=ve_c[t][:], in0=mv_c[t][:, 1:2], scalar1=EPS, scalar2=1.0, op0=ALU.add, op1=ALU.mult
-            )
-            nc.gpsimd.tensor_tensor(out=rs_c[t][:], in0=ve_c[t][:], in1=neghalf[:, 0:1], op=ALU.pow)
-            nc.vector.scalar_tensor_tensor(
-                out=a_c[t][:], in0=cc[t][:], scalar=mv_c[t][:, 0:1], in1=wc_sb[:], op0=ALU.subtract, op1=ALU.mult
-            )
-
-        def cell_out(t):
-            nc.vector.scalar_tensor_tensor(
-                out=acy[t][:], in0=a_c[t][:], scalar=rs_c[t][:], in1=bc_sb[:], op0=ALU.mult, op1=ALU.add
-            )
-            nc.sync.dma_start(out=o1_v[:, t, :], in_=acy[t][:])
-            nc.scalar.activation(out=th[t][:], in_=acy[t][:], func=ACT.Tanh)
-
-        def hidden_out(t):
-            nc.vector.tensor_tensor(out=ada[t][:], in0=sg[t][:, 3 * AH : 4 * AH], in1=th[t][:], op=ALU.mult)
-            nc.sync.dma_start(out=o0_v[:, t, :], in_=ada[t][:])
-
         ahT_ps = tp.tile([P, NT * P], BF16, tag="tp")
         for t in range(NT):
             nc.tensor.transpose(ahT_ps[:, t * P : (t + 1) * P], ah_sb[:, t * AH : (t + 1) * AH], ident_b[:])
-        nc.vector.tensor_copy(out=ahT[:], in_=ahT_ps[:])
         whhT_ps = tp.tile([P, N], BF16, tag="tp")
         for j in range(G):
             nc.tensor.transpose(whhT_ps[:, j * P : (j + 1) * P], whh_sb[:, j, :], ident_b[:])
+        nc.vector.tensor_copy(out=ahT[:], in_=ahT_ps[:])
         nc.scalar.copy(out=whhT[:], in_=whhT_ps[:])
-        vT_ps = tp.tile([P, P], BF16, tag="tp")
-        nc.tensor.transpose(vT_ps[:], vrows[:], ident_b[:])
-        nc.vector.tensor_copy(out=vcol[:], in_=vT_ps[:, 0:16])
-        nc.vector.tensor_add(out=bsum[:], in0=vcol[:, 4:8], in1=vcol[:, 12:16])
-        spread_cols = (vcol[:, 8:12], bsum[:], vcol[:, 0:4])
 
+        hg_ps = []
         for j in range(G):
             banks = [transposed_bank(w_sb[j], h) for h in range(2)]
             for h in range(2):
                 nc.scalar.copy(out=wgrp_f[:, 2 * h : 2 * h + 2, j, :, :], in_=banks[h])
             if j == 0:
                 for t in range(NT):
-                    hg_ps[t] = acc.tile([P, N], F32, name="hg_ps", tag="acc")
-                    nc.tensor.matmul(hg_ps[t][:], lhsT=ahT[:, t * P : (t + 1) * P], rhs=whhT[:], start=True, stop=True)
-            if j < 3:
-                spread(spread_cols[j], gains[j])
-            if j == 0:
-                for t in range(NT):
-                    nc.vector.bn_stats(out=st_h[t][:], in_=hg_ps[t][:])
-                    nc.vector.bn_aggr(out=mv_h[:, t, :], in_=st_h[t][:])
-                nc.gpsimd.tensor_scalar(
-                    out=ve_h[:], in0=mv_h[:, :, 1], scalar1=EPS, scalar2=1.0, op0=ALU.add, op1=ALU.mult
-                )
-                nc.gpsimd.tensor_tensor(out=rs_h[:], in0=ve_h[:], in1=neghalf[:], op=ALU.pow)
-            if j == 1:
-                hg_centre(0)
-                hg_centre(1)
-            if j == 2:
-                hg_scale(0)
-                hg_scale(1)
+                    hg = acc.tile([P, N], F32, name="hg", tag="acc")
+                    nc.tensor.matmul(hg[:], lhsT=ahT[:, t * P : (t + 1) * P], rhs=whhT[:], start=True, stop=True)
+                    hg_ps.append(hg)
+                for i, dst in enumerate((Wh, Bs)):
+                    ps = tp.tile([P, N], F32, name="ps_s", tag="tp")
+                    nc.tensor.matmul(ps[:], lhsT=ones[:], rhs=rows[:, i * N : (i + 1) * N], start=True, stop=True)
+                    nc.scalar.copy(out=dst[:], in_=ps[:])
+                mean_var(ln_h, [hg[:] for hg in hg_ps])
+                rstd(ln_h, 0, NT)
             if j % 2 == 1:
+                for t in (j - 1, j):
+                    centre_gain(a_h[t][:], hg_ps[t][:], ln_h, t, Wh[:])
                 for g in range(NG):
                     quantise(w_codes, w_scales, wgrp, g * N + (j - 1) * P, 2 * P)
 
-        def live(t):
-            return 0 <= t < NT
+        ig_ps = []
+        for s in range(NT + 2):
+            if s < NT:
+                banks = [transposed_bank(a_sb[s], h) for h in range(2)]
+                agrp_f = agrp[s][:].bitcast(F32).rearrange("p (g r u) -> p g r u", g=NG, u=2)
+                for h in range(2):
+                    nc.scalar.copy(out=agrp_f[:, 2 * h : 2 * h + 2, :, :], in_=banks[h])
+            if s >= 2:
+                t = s - 2
+                for h in range(2):
+                    quantise(a_codes[t], a_scales[t], agrp[t], h * 2 * P, 2 * P)
+                ig = acc.tile([P, N], F32, name="ig", tag="acc")
+                for g in range(NG):
+                    nc.tensor.matmul_mx(
+                        out=ig[:],
+                        lhsT=a_codes[t][:, g * P : (g + 1) * P].bitcast(FP8X4),
+                        lhsT_scale=a_scales[t][:, g * P : (g + 1) * P],
+                        rhs=w_codes[:, g * N : (g + 1) * N].bitcast(FP8X4),
+                        rhs_scale=w_scales[:, g * N : (g + 1) * N],
+                        start=(g == 0),
+                        stop=(g == NG - 1),
+                    )
+                ig_ps.append(ig)
+                scale_shift(h_t[t][:], a_h[t][:], ln_h, t, Bs[:])
 
-        for r in range(-4, NT + 4):
-            if live(r):
-                ig_stats(r)
-            if live(r + 4):
-                a_transpose(r + 4)
-            if live(r + 3):
-                a_copy(r + 3)
-            if r in (-2, -1):
-                hg_centre(r + 4)
-                hg_scale(r + 4)
-            if live(r + 2):
-                a_multiply(r + 2)
-            if live(r - 2):
-                cell(r - 2)
-            if live(r - 1):
-                gates(r - 1)
-            if live(r - 3):
-                cell_out(r - 3)
-            if live(r):
-                ig_centre(r)
-            if live(r - 4):
-                hidden_out(r - 4)
+        mean_var(ln_i, [ig[:] for ig in ig_ps])
+        rstd(ln_i, 0, NT)
+        for t in range(NT):
+            centre_gain(a_i[t][:], ig_ps[t][:], ln_i, t, Wi[:])
+        for t in range(NT):
+            scale_shift(gt[t][:], a_i[t][:], ln_i, t, h_t[t][:])
+            nc.scalar.activation(out=sg[:, t, 0 : 2 * AH], in_=gt[t][:, 0 : 2 * AH], func=ACT.Sigmoid)
+            nc.scalar.activation(out=sg[:, t, 2 * AH : 3 * AH], in_=gt[t][:, 2 * AH : 3 * AH], func=ACT.Tanh)
+            nc.scalar.activation(out=sg[:, t, 3 * AH : 4 * AH], in_=gt[t][:, 3 * AH : 4 * AH], func=ACT.Sigmoid)
+
+        halves = (slice(0, 2), slice(2, 4))
+        half_tiles = ((0, 1), (2, 3))
+        for hf in halves:
+            nc.vector.tensor_tensor(out=m1[:, hf, :], in0=sg[:, hf, AH : 2 * AH], in1=ac_sb[:, hf, :], op=ALU.mult)
+            nc.vector.tensor_tensor(out=m2[:, hf, :], in0=sg[:, hf, 0:AH], in1=sg[:, hf, 2 * AH : 3 * AH], op=ALU.mult)
+        for hf in halves:
+            nc.vector.tensor_tensor(out=cc[:, hf, :], in0=m1[:, hf, :], in1=m2[:, hf, :], op=ALU.add)
+        mean_var(ln_c, [cc[:, t, :] for t in range(NT)])
+        rstd(ln_c, 0, 2)
+        rstd(ln_c, 2, 4)
+        for t in range(NT):
+            centre_gain(a_c[:, t, :], cc[:, t, :], ln_c, t, Wc[:])
+        for hf, tiles in zip(halves, half_tiles):
+            for t in tiles:
+                scale_shift(acy[:, t, :], a_c[:, t, :], ln_c, t, Bc[:])
+            nc.sync.dma_start(out=o1_v[:, hf, :], in_=acy[:, hf, :])
+            nc.scalar.activation(out=th[:, hf, :], in_=acy[:, hf, :], func=ACT.Tanh)
+        for hf in halves:
+            nc.vector.tensor_tensor(out=ada[:, hf, :], in0=sg[:, hf, 3 * AH : 4 * AH], in1=th[:, hf, :], op=ALU.mult)
+            nc.sync.dma_start(out=o0_v[:, hf, :], in_=ada[:, hf, :])

@@ -42,6 +42,8 @@ def tile_adaptivelstmcell_pa_kernel(
         nc.vector.memset(warm[:], 0.0)
         neghalf = sb.tile([P, NT], F32)
         nc.vector.memset(neghalf[:], -0.5)
+        eps_t = sb.tile([P, 1], F32)
+        nc.vector.memset(eps_t[:], EPS)
         ident_b = sb.tile([P, P], BF16)
         make_identity(nc, ident_b[:])
         ident_f = sb.tile([P, P], F32)
@@ -91,7 +93,14 @@ def tile_adaptivelstmcell_pa_kernel(
         a_h = per_tile([P, N], F32, "a_h")
         h_t = per_tile([P, N], F32, "h_t")
         a_i = per_tile([P, N], F32, "a_i")
-        gt = per_tile([P, N], F32, "gt")
+        gt = sb.tile([P, NT, N], F32)
+        v_i = [sb.tile([P, N], F32, name="v_i%d" % t) for t in range(2)]
+        junk = sb.tile([P, N], BF16)
+        sum_a = sb.tile([P, 2], F32)
+        nm_a = sb.tile([P, 2], F32)
+        ssq_a = sb.tile([P, 2], F32)
+        ve_a = sb.tile([P, 2], F32)
+        rs_a = sb.tile([P, 2], F32)
         sg = sb.tile([P, NT, N], F32)
         m1 = sb.tile([P, NT, AH], F32)
         m2 = sb.tile([P, NT, AH], F32)
@@ -104,18 +113,18 @@ def tile_adaptivelstmcell_pa_kernel(
         o1_v = out_1.rearrange("(p t) c -> p t c", t=NT)
 
         def norm_tiles(name):
-            st = per_tile([P, 6], F32, "st_" + name)
+            st = sb.tile([P, NT, 6], F32, name="st_" + name)
             mv = sb.tile([P, NT, 2], F32, name="mv_" + name)
             ve = sb.tile([P, NT], F32, name="ve_" + name)
             rs = sb.tile([P, NT], F32, name="rs_" + name)
             return st, mv, ve, rs
 
-        def mean_var(tiles, srcs):
+        def mean_var(tiles, srcs, t0=0):
             st, mv, ve, rs = tiles
-            for t in range(NT):
-                nc.vector.bn_stats(out=st[t][:], in_=srcs[t])
-            for t in range(NT):
-                nc.vector.bn_aggr(out=mv[:, t, :], in_=st[t][:])
+            for t in range(t0, NT):
+                nc.vector.bn_stats(out=st[:, t, :], in_=srcs[t])
+            for t in range(t0, NT):
+                nc.vector.bn_aggr(out=mv[:, t, :], in_=st[:, t, :])
 
         def rstd(tiles, t0, t1):
             st, mv, ve, rs = tiles
@@ -176,9 +185,10 @@ def tile_adaptivelstmcell_pa_kernel(
                     nc.scalar.copy(out=dst[:], in_=ps[:])
                 mean_var(ln_h, [hg[:] for hg in hg_ps])
                 rstd(ln_h, 0, NT)
-            if j % 2 == 1:
-                for t in (j - 1, j):
+            if j == 1:
+                for t in (0, 1):
                     centre_gain(a_h[t][:], hg_ps[t][:], ln_h, t, Wh[:])
+            if j % 2 == 1:
                 for g in range(NG):
                     quantise(w_codes, w_scales, wgrp, g * N + (j - 1) * P, 2 * P)
 
@@ -205,17 +215,41 @@ def tile_adaptivelstmcell_pa_kernel(
                         stop=(g == NG - 1),
                     )
                 ig_ps.append(ig)
+                if t + 2 < NT:
+                    centre_gain(a_h[t + 2][:], hg_ps[t + 2][:], ln_h, t + 2, Wh[:])
                 scale_shift(h_t[t][:], a_h[t][:], ln_h, t, Bs[:])
+            if s in (3, 4):
+                u = s - 3
+                nc.scalar.activation(out=v_i[u][:], in_=ig_ps[u][:], func=ACT.Identity, accum_out=sum_a[:, u : u + 1])
+            if s == 4:
+                nc.scalar.mul(out=nm_a[:], in_=sum_a[:], mul=-1.0 / N)
+                for u in range(2):
+                    nc.scalar.activation(
+                        out=junk[:], in_=v_i[u][:], func=ACT.Square, bias=nm_a[:, u : u + 1], accum_out=ssq_a[:, u : u + 1]
+                    )
+                nc.scalar.activation(out=ve_a[:], in_=ssq_a[:], func=ACT.Identity, scale=1.0 / N, bias=eps_t[:])
+                nc.gpsimd.tensor_tensor(out=rs_a[:], in0=ve_a[:], in1=neghalf[:, 0:2], op=ALU.pow)
 
-        mean_var(ln_i, [ig[:] for ig in ig_ps])
-        rstd(ln_i, 0, NT)
-        for t in range(NT):
+        def gates(t, rs_col):
+            nc.vector.scalar_tensor_tensor(
+                out=gt[:, t, :], in0=a_i[t][:], scalar=rs_col, in1=h_t[t][:], op0=ALU.mult, op1=ALU.add
+            )
+            nc.scalar.activation(out=sg[:, t, 0 : 2 * AH], in_=gt[:, t, 0 : 2 * AH], func=ACT.Sigmoid)
+            nc.scalar.activation(out=sg[:, t, 2 * AH : 3 * AH], in_=gt[:, t, 2 * AH : 3 * AH], func=ACT.Tanh)
+
+        for t in range(2):
+            nc.vector.scalar_tensor_tensor(
+                out=a_i[t][:], in0=v_i[t][:], scalar=nm_a[:, t : t + 1], in1=Wi[:], op0=ALU.add, op1=ALU.mult
+            )
+        mean_var(ln_i, [ig[:] for ig in ig_ps], 2)
+        rstd(ln_i, 2, NT)
+        for t in range(2):
+            gates(t, rs_a[:, t : t + 1])
+        for t in range(2, NT):
             centre_gain(a_i[t][:], ig_ps[t][:], ln_i, t, Wi[:])
-        for t in range(NT):
-            scale_shift(gt[t][:], a_i[t][:], ln_i, t, h_t[t][:])
-            nc.scalar.activation(out=sg[:, t, 0 : 2 * AH], in_=gt[t][:, 0 : 2 * AH], func=ACT.Sigmoid)
-            nc.scalar.activation(out=sg[:, t, 2 * AH : 3 * AH], in_=gt[t][:, 2 * AH : 3 * AH], func=ACT.Tanh)
-            nc.scalar.activation(out=sg[:, t, 3 * AH : 4 * AH], in_=gt[t][:, 3 * AH : 4 * AH], func=ACT.Sigmoid)
+        for t in range(2, NT):
+            gates(t, ln_i[3][:, t : t + 1])
+        nc.scalar.activation(out=sg[:, :, 3 * AH : 4 * AH], in_=gt[:, :, 3 * AH : 4 * AH], func=ACT.Sigmoid)
 
         halves = (slice(0, 2), slice(2, 4))
         half_tiles = ((0, 1), (2, 3))

@@ -42,8 +42,6 @@ def tile_adaptivelstmcell_pa_kernel(
         nc.vector.memset(warm[:], 0.0)
         neghalf = sb.tile([P, NT], F32)
         nc.vector.memset(neghalf[:], -0.5)
-        eps_t = sb.tile([P, 1], F32)
-        nc.vector.memset(eps_t[:], EPS)
         ident_b = sb.tile([P, P], BF16)
         make_identity(nc, ident_b[:])
         ident_f = sb.tile([P, P], F32)
@@ -94,13 +92,6 @@ def tile_adaptivelstmcell_pa_kernel(
         h_t = per_tile([P, N], F32, "h_t")
         a_i = per_tile([P, N], F32, "a_i")
         gt = sb.tile([P, NT, N], F32)
-        v_i = [sb.tile([P, N], F32, name="v_i%d" % t) for t in range(2)]
-        junk = sb.tile([P, N], BF16)
-        sum_a = sb.tile([P, 2], F32)
-        nm_a = sb.tile([P, 2], F32)
-        ssq_a = sb.tile([P, 2], F32)
-        ve_a = sb.tile([P, 2], F32)
-        rs_a = sb.tile([P, 2], F32)
         sg = sb.tile([P, NT, N], F32)
         m1 = sb.tile([P, NT, AH], F32)
         m2 = sb.tile([P, NT, AH], F32)
@@ -113,18 +104,18 @@ def tile_adaptivelstmcell_pa_kernel(
         o1_v = out_1.rearrange("(p t) c -> p t c", t=NT)
 
         def norm_tiles(name):
-            st = sb.tile([P, NT, 6], F32, name="st_" + name)
+            st = per_tile([P, 6], F32, "st_" + name)
             mv = sb.tile([P, NT, 2], F32, name="mv_" + name)
             ve = sb.tile([P, NT], F32, name="ve_" + name)
             rs = sb.tile([P, NT], F32, name="rs_" + name)
             return st, mv, ve, rs
 
-        def mean_var(tiles, srcs, t0=0):
+        def mean_var(tiles, srcs):
             st, mv, ve, rs = tiles
-            for t in range(t0, NT):
-                nc.vector.bn_stats(out=st[:, t, :], in_=srcs[t])
-            for t in range(t0, NT):
-                nc.vector.bn_aggr(out=mv[:, t, :], in_=st[:, t, :])
+            for t in range(NT):
+                nc.vector.bn_stats(out=st[t][:], in_=srcs[t])
+            for t in range(NT):
+                nc.vector.bn_aggr(out=mv[:, t, :], in_=st[t][:])
 
         def rstd(tiles, t0, t1):
             st, mv, ve, rs = tiles
@@ -185,10 +176,9 @@ def tile_adaptivelstmcell_pa_kernel(
                     nc.scalar.copy(out=dst[:], in_=ps[:])
                 mean_var(ln_h, [hg[:] for hg in hg_ps])
                 rstd(ln_h, 0, NT)
-            if j == 1:
-                for t in (0, 1):
-                    centre_gain(a_h[t][:], hg_ps[t][:], ln_h, t, Wh[:])
             if j % 2 == 1:
+                for t in (j - 1, j):
+                    centre_gain(a_h[t][:], hg_ps[t][:], ln_h, t, Wh[:])
                 for g in range(NG):
                     quantise(w_codes, w_scales, wgrp, g * N + (j - 1) * P, 2 * P)
 
@@ -215,41 +205,20 @@ def tile_adaptivelstmcell_pa_kernel(
                         stop=(g == NG - 1),
                     )
                 ig_ps.append(ig)
-                if t + 2 < NT:
-                    centre_gain(a_h[t + 2][:], hg_ps[t + 2][:], ln_h, t + 2, Wh[:])
                 scale_shift(h_t[t][:], a_h[t][:], ln_h, t, Bs[:])
-            if s in (3, 4):
-                u = s - 3
-                nc.scalar.activation(out=v_i[u][:], in_=ig_ps[u][:], func=ACT.Identity, accum_out=sum_a[:, u : u + 1])
-            if s == 4:
-                nc.scalar.mul(out=nm_a[:], in_=sum_a[:], mul=-1.0 / N)
-                for u in range(2):
-                    nc.scalar.activation(
-                        out=junk[:], in_=v_i[u][:], func=ACT.Square, bias=nm_a[:, u : u + 1], accum_out=ssq_a[:, u : u + 1]
-                    )
-                nc.scalar.activation(out=ve_a[:], in_=ssq_a[:], func=ACT.Identity, scale=1.0 / N, bias=eps_t[:])
-                nc.gpsimd.tensor_tensor(out=rs_a[:], in0=ve_a[:], in1=neghalf[:, 0:2], op=ALU.pow)
 
-        def gates(t, rs_col):
-            nc.vector.scalar_tensor_tensor(
-                out=gt[:, t, :], in0=a_i[t][:], scalar=rs_col, in1=h_t[t][:], op0=ALU.mult, op1=ALU.add
-            )
-            nc.scalar.activation(out=sg[:, t, 0 : 2 * AH], in_=gt[:, t, 0 : 2 * AH], func=ACT.Sigmoid)
-            nc.scalar.activation(out=sg[:, t, 2 * AH : 3 * AH], in_=gt[:, t, 2 * AH : 3 * AH], func=ACT.Tanh)
+        mean_var(ln_i, [ig[:] for ig in ig_ps])
+        rstd(ln_i, 0, NT)
+        def gate_inputs(cols, act):
+            for t in range(NT):
+                centre_gain(a_i[t][:, cols], ig_ps[t][:, cols], ln_i, t, Wi[:, cols])
+            for t in range(NT):
+                scale_shift(gt[:, t, cols], a_i[t][:, cols], ln_i, t, h_t[t][:, cols])
+                if act:
+                    nc.scalar.activation(out=sg[:, t, 0 : 2 * AH], in_=gt[:, t, 0 : 2 * AH], func=ACT.Sigmoid)
+                    nc.scalar.activation(out=sg[:, t, 2 * AH : 3 * AH], in_=gt[:, t, 2 * AH : 3 * AH], func=ACT.Tanh)
 
-        for t in range(2):
-            nc.vector.scalar_tensor_tensor(
-                out=a_i[t][:], in0=v_i[t][:], scalar=nm_a[:, t : t + 1], in1=Wi[:], op0=ALU.add, op1=ALU.mult
-            )
-        mean_var(ln_i, [ig[:] for ig in ig_ps], 2)
-        rstd(ln_i, 2, NT)
-        for t in range(2):
-            gates(t, rs_a[:, t : t + 1])
-        for t in range(2, NT):
-            centre_gain(a_i[t][:], ig_ps[t][:], ln_i, t, Wi[:])
-        for t in range(2, NT):
-            gates(t, ln_i[3][:, t : t + 1])
-        nc.scalar.activation(out=sg[:, :, 3 * AH : 4 * AH], in_=gt[:, :, 3 * AH : 4 * AH], func=ACT.Sigmoid)
+        gate_inputs(slice(0, 3 * AH), True)
 
         halves = (slice(0, 2), slice(2, 4))
         half_tiles = ((0, 1), (2, 3))
@@ -259,8 +228,9 @@ def tile_adaptivelstmcell_pa_kernel(
         for hf in halves:
             nc.vector.tensor_tensor(out=cc[:, hf, :], in0=m1[:, hf, :], in1=m2[:, hf, :], op=ALU.add)
         mean_var(ln_c, [cc[:, t, :] for t in range(NT)])
-        rstd(ln_c, 0, 2)
-        rstd(ln_c, 2, 4)
+        rstd(ln_c, 0, NT)
+        gate_inputs(slice(3 * AH, 4 * AH), False)
+        nc.scalar.activation(out=sg[:, :, 3 * AH : 4 * AH], in_=gt[:, :, 3 * AH : 4 * AH], func=ACT.Sigmoid)
         for t in range(NT):
             centre_gain(a_c[:, t, :], cc[:, t, :], ln_c, t, Wc[:])
         for hf, tiles in zip(halves, half_tiles):

@@ -34,12 +34,12 @@ def tile_adaptivelstmcell_pa_kernel(
         def per_tile(shape, dtype, name, align=None):
             return [sb.tile(shape, dtype, name="%s%d" % (name, t), align_bytes=align) for t in range(NT)]
 
-        rows = sb.tile([P, 2 * N], BF16)
-        nc.vector.memset(rows[:], 0.0)
-        ones = sb.tile([P, P], BF16)
-        nc.vector.memset(ones[:], 1.0)
         warm = sb.tile([P, 1], F32)
         nc.vector.memset(warm[:], 0.0)
+        rows = sb.tile([P, 2 * N], BF16)
+        nc.vector.memset(rows[:].bitcast(F32), 0.0)
+        ones = sb.tile([P, P], BF16)
+        nc.vector.memset(ones[:], 1.0)
         neghalf = sb.tile([P, NT], F32)
         nc.vector.memset(neghalf[:], -0.5)
         ident_b = sb.tile([P, P], BF16)
@@ -54,11 +54,11 @@ def tile_adaptivelstmcell_pa_kernel(
         nc.sync.dma_start(out=ah_sb[:], in_=ah.rearrange("(p t) k -> p (t k)", t=NT))
         whh_sb = sb.tile([P, G, AH], BF16)
         nc.sync.dma_start(out=whh_sb[:], in_=a_w_hh.rearrange("(j p) k -> p j k", p=P))
+        warm2 = sb.tile([P, 1], F32)
+        nc.scalar.activation(out=warm2[:], in_=warm[:], func=ACT.Sigmoid)
         nc.scalar.dma_start(out=rows[0:1, 0:N], in_=as_row(a_ln_h_w))
         nc.scalar.dma_start(out=rows[0:1, N : 2 * N], in_=as_row(a_ln_i_b))
         nc.scalar.dma_start(out=rows[1:2, N : 2 * N], in_=as_row(a_ln_h_b))
-        warm2 = sb.tile([P, 1], F32)
-        nc.scalar.activation(out=warm2[:], in_=warm[:], func=ACT.Sigmoid)
         w_sb = per_tile([P, K], BF16, "w_sb")
         for j in range(G):
             nc.sync.dma_start(out=w_sb[j][:], in_=a_w_ih[j * P : (j + 1) * P, :])
@@ -158,18 +158,24 @@ def tile_adaptivelstmcell_pa_kernel(
         for j in range(G):
             nc.tensor.transpose(whhT_ps[:, j * P : (j + 1) * P], whh_sb[:, j, :], ident_b[:])
         nc.vector.tensor_copy(out=ahT[:], in_=ahT_ps[:])
-        nc.scalar.copy(out=whhT[:], in_=whhT_ps[:])
+        nc.vector.tensor_copy(out=whhT[:], in_=whhT_ps[:])
 
         hg_ps = []
+
+        def hidden_product(t):
+            hg = acc.tile([P, N], F32, name="hg", tag="acc")
+            nc.tensor.matmul(hg[:], lhsT=ahT[:, t * P : (t + 1) * P], rhs=whhT[:], start=True, stop=True)
+            hg_ps.append(hg)
+
+        hidden_product(0)
+        hidden_product(1)
         for j in range(G):
             banks = [transposed_bank(w_sb[j], h) for h in range(2)]
             for h in range(2):
                 nc.scalar.copy(out=wgrp_f[:, 2 * h : 2 * h + 2, j, :, :], in_=banks[h])
             if j == 0:
-                for t in range(NT):
-                    hg = acc.tile([P, N], F32, name="hg", tag="acc")
-                    nc.tensor.matmul(hg[:], lhsT=ahT[:, t * P : (t + 1) * P], rhs=whhT[:], start=True, stop=True)
-                    hg_ps.append(hg)
+                hidden_product(2)
+                hidden_product(3)
                 for i, dst in enumerate((Wh, Bs)):
                     ps = tp.tile([P, N], F32, name="ps_s", tag="tp")
                     nc.tensor.matmul(ps[:], lhsT=ones[:], rhs=rows[:, i * N : (i + 1) * N], start=True, stop=True)

@@ -40,6 +40,8 @@ def tile_adaptivelstmcell_pa_kernel(
         nc.vector.memset(rows[:].bitcast(F32), 0.0)
         ones = sb.tile([P, P], BF16)
         nc.vector.memset(ones[:], 1.0)
+        eps = sb.tile([P, 1], F32)
+        nc.vector.memset(eps[:], EPS)
         neghalf = sb.tile([P, NT], F32)
         nc.vector.memset(neghalf[:], -0.5)
         ident_b = sb.tile([P, P], BF16)
@@ -55,7 +57,7 @@ def tile_adaptivelstmcell_pa_kernel(
         whh_sb = sb.tile([P, G, AH], BF16)
         nc.sync.dma_start(out=whh_sb[:], in_=a_w_hh.rearrange("(j p) k -> p j k", p=P))
         warm2 = sb.tile([P, 1], F32)
-        nc.scalar.activation(out=warm2[:], in_=warm[:], func=ACT.Sigmoid)
+        nc.scalar.activation(out=warm2[:], in_=warm[:], func=ACT.Sqrt)
         nc.scalar.dma_start(out=rows[0:1, 0:N], in_=as_row(a_ln_h_w))
         nc.scalar.dma_start(out=rows[0:1, N : 2 * N], in_=as_row(a_ln_i_b))
         nc.scalar.dma_start(out=rows[1:2, N : 2 * N], in_=as_row(a_ln_h_b))
@@ -70,17 +72,34 @@ def tile_adaptivelstmcell_pa_kernel(
             nc.sync.dma_start(out=a_sb[t][:, I:K], in_=hx_v[:, t, :])
         ac_sb = sb.tile([P, NT, AH], BF16)
         nc.sync.dma_start(out=ac_sb[:], in_=ac.rearrange("(p t) c -> p t c", t=NT))
-        Wi = sb.tile([P, N], BF16)
-        nc.sync.dma_start(out=Wi[:], in_=a_ln_i_w.partition_broadcast(P))
+        main, last = slice(0, 3 * AH), slice(3 * AH, N)
+        Wi = sb.tile([P, 3 * AH], BF16)
+        nc.sync.dma_start(out=Wi[:], in_=a_ln_i_w[main].partition_broadcast(P))
         Wc = sb.tile([P, AH], BF16)
         nc.sync.dma_start(out=Wc[:], in_=a_ln_c_w.partition_broadcast(P))
         Bc = sb.tile([P, AH], BF16)
         nc.sync.dma_start(out=Bc[:], in_=a_ln_c_b.partition_broadcast(P))
+        o_raw = []
+        for v, vec in enumerate((a_ln_h_w, a_ln_i_w, a_ln_i_b, a_ln_h_b)):
+            col = sb.tile([P, 2], BF16, name="o_raw%d" % v)
+            nc.sync.dma_start(out=col[:, 0:1], in_=vec[last].rearrange("(p o) -> p o", o=1))
+            o_raw.append(col)
 
         ahT = sb.tile([P, NT * P], BF16)
         whhT = sb.tile([P, N], BF16)
         Wh = sb.tile([P, N], F32)
         Bs = sb.tile([P, N], F32)
+        o_gain = sb.tile([P, 2], F32)
+        o_bias = sb.tile([P, 1], F32)
+        z_ho = per_tile([P, AH], F32, "z_ho")
+        z_io = per_tile([P, AH], F32, "z_io")
+        h_o = sb.tile([P, NT * P], F32)
+        g_o = sb.tile([P, NT * P], F32)
+        s_o = sb.tile([P, NT * P], F32)
+        junk = per_tile([P, N], F32, "junk")
+        nmean = sb.tile([P, 2], F32)
+        ssd = sb.tile([P, 2], F32)
+        nb = sb.tile([P, NT], F32)
         wgrp = sb.tile([P, NG * N * 4], BF16, align_bytes=64)
         wgrp_f = wgrp[:].bitcast(F32).rearrange("p (g j r u) -> p g j r u", g=NG, j=G, u=2)
         w_codes = sb.tile([P, NG * N], U32, align_bytes=64)
@@ -88,11 +107,11 @@ def tile_adaptivelstmcell_pa_kernel(
         agrp = per_tile([P, NG * P * 4], BF16, "agrp", 64)
         a_codes = per_tile([P, NG * P], U32, "a_codes", 64)
         a_scales = per_tile([P, NG * P], U8, "a_scales", 64)
-        a_h = per_tile([P, N], F32, "a_h")
-        h_t = per_tile([P, N], F32, "h_t")
-        a_i = per_tile([P, N], F32, "a_i")
-        gt = sb.tile([P, NT, N], F32)
-        sg = sb.tile([P, NT, N], F32)
+        a_h = per_tile([P, 3 * AH], F32, "a_h")
+        h_t = per_tile([P, 3 * AH], F32, "h_t")
+        a_i = per_tile([P, 3 * AH], F32, "a_i")
+        gt = sb.tile([P, NT, 3 * AH], F32)
+        sg = sb.tile([P, NT, 3 * AH], F32)
         m1 = sb.tile([P, NT, AH], F32)
         m2 = sb.tile([P, NT, AH], F32)
         cc = sb.tile([P, NT, AH], F32)
@@ -121,6 +140,12 @@ def tile_adaptivelstmcell_pa_kernel(
             st, mv, ve, rs = tiles
             nc.vector.tensor_scalar_add(out=ve[:, t0:t1], in0=mv[:, t0:t1, 1], scalar1=EPS)
             nc.gpsimd.tensor_tensor(out=rs[:, t0:t1], in0=ve[:, t0:t1], in1=neghalf[:, t0:t1], op=ALU.pow)
+
+        def std(tiles, t0, t1, var, scale=1.0):
+            nc.scalar.activation(out=tiles[2][:, t0:t1], in_=var, func=ACT.Sqrt, scale=scale, bias=eps[:])
+
+        def inverse(tiles, t0, t1):
+            nc.vector.reciprocal(out=tiles[3][:, t0:t1], in_=tiles[2][:, t0:t1])
 
         def centre_gain(out, src, tiles, t, gain):
             nc.vector.scalar_tensor_tensor(
@@ -160,6 +185,13 @@ def tile_adaptivelstmcell_pa_kernel(
         nc.vector.tensor_copy(out=ahT[:], in_=ahT_ps[:])
         nc.vector.tensor_copy(out=whhT[:], in_=whhT_ps[:])
 
+        def norm_ho(tiles):
+            for t in tiles:
+                nc.vector.tensor_scalar(
+                    out=z_ho[t][:], in0=hg_ps[t][:, last], scalar1=ln_h[1][:, t, 0:1], scalar2=ln_h[3][:, t : t + 1],
+                    op0=ALU.subtract, op1=ALU.mult,
+                )
+
         hg_ps = []
 
         def hidden_product(t):
@@ -181,12 +213,15 @@ def tile_adaptivelstmcell_pa_kernel(
                     nc.tensor.matmul(ps[:], lhsT=ones[:], rhs=rows[:, i * N : (i + 1) * N], start=True, stop=True)
                     nc.scalar.copy(out=dst[:], in_=ps[:])
                 mean_var(ln_h, [hg[:] for hg in hg_ps])
-                rstd(ln_h, 0, NT)
+                std(ln_h, 0, NT, ln_h[1][:, :, 1])
             if j % 2 == 1:
                 for t in (j - 1, j):
-                    centre_gain(a_h[t][:], hg_ps[t][:], ln_h, t, Wh[:])
+                    centre_gain(a_h[t][:], hg_ps[t][:, main], ln_h, t, Wh[:, main])
                 for g in range(NG):
                     quantise(w_codes, w_scales, wgrp, g * N + (j - 1) * P, 2 * P)
+                if j == 1:
+                    inverse(ln_h, 0, NT)
+                    norm_ho((0, 1))
 
         ig_ps = []
         for s in range(NT + 2):
@@ -211,39 +246,121 @@ def tile_adaptivelstmcell_pa_kernel(
                         stop=(g == NG - 1),
                     )
                 ig_ps.append(ig)
-                scale_shift(h_t[t][:], a_h[t][:], ln_h, t, Bs[:])
+                if t == 0:
+                    norm_ho((2, 3))
+                scale_shift(h_t[t][:], a_h[t][:], ln_h, t, Bs[:, main])
 
-        mean_var(ln_i, [ig[:] for ig in ig_ps])
-        rstd(ln_i, 0, NT)
-        def gate_inputs(cols, act):
+        def turned_o(tiles):
+            ps = tp.tile([P, NT * P], F32, name="ps_o", tag="tp")
             for t in range(NT):
-                centre_gain(a_i[t][:, cols], ig_ps[t][:, cols], ln_i, t, Wi[:, cols])
-            for t in range(NT):
-                scale_shift(gt[:, t, cols], a_i[t][:, cols], ln_i, t, h_t[t][:, cols])
-                if act:
-                    nc.scalar.activation(out=sg[:, t, 0 : 2 * AH], in_=gt[:, t, 0 : 2 * AH], func=ACT.Sigmoid)
-                    nc.scalar.activation(out=sg[:, t, 2 * AH : 3 * AH], in_=gt[:, t, 2 * AH : 3 * AH], func=ACT.Tanh)
+                nc.tensor.transpose(ps[:, t * P : (t + 1) * P], tiles[t], ident_f[:])
+            return ps
 
-        gate_inputs(slice(0, 3 * AH), True)
+        for v in range(2):
+            nc.vector.tensor_copy(out=o_gain[:, v : v + 1], in_=o_raw[v][:, 0:1])
+        nc.vector.tensor_tensor(out=o_bias[:], in0=o_raw[2][:, 0:1], in1=o_raw[3][:, 0:1], op=ALU.add)
+        ho_ps = turned_o([z[:] for z in z_ho])
+
+        for t in range(2):
+            nc.scalar.activation(
+                out=junk[t][:], in_=ig_ps[t][:], func=ACT.Identity, scale=-1.0 / N, accum_out=nmean[:, t : t + 1]
+            )
+        for t in range(2):
+            nc.scalar.activation(
+                out=junk[2 + t][:], in_=ig_ps[t][:], func=ACT.Square, bias=nmean[:, t : t + 1], accum_out=ssd[:, t : t + 1]
+            )
+        nc.scalar.activation(out=h_o[:], in_=ho_ps[:], func=ACT.Identity, scale=o_gain[:, 0:1], bias=o_bias[:])
+
+        def centre_i(t):
+            if t < 2:
+                nc.vector.scalar_tensor_tensor(
+                    out=a_i[t][:], in0=ig_ps[t][:, main], scalar=nmean[:, t : t + 1], in1=Wi[:], op0=ALU.add, op1=ALU.mult
+                )
+            else:
+                centre_gain(a_i[t][:], ig_ps[t][:, main], ln_i, t, Wi[:])
+
+        st_i, mv_i, ve_i, rs_i = ln_i
+
+        def gates(t):
+            scale_shift(gt[:, t, :], a_i[t][:], ln_i, t, h_t[t][:])
+            nc.scalar.activation(out=sg[:, t, 0 : 2 * AH], in_=gt[:, t, 0 : 2 * AH], func=ACT.Sigmoid)
+            nc.scalar.activation(out=sg[:, t, 2 * AH : 3 * AH], in_=gt[:, t, 2 * AH : 3 * AH], func=ACT.Tanh)
+
+        std(ln_i, 0, 2, ssd[:], 1.0 / N)
+        nc.vector.bn_stats(out=st_i[2][:], in_=ig_ps[2][:])
+        centre_i(0)
+        nc.vector.bn_aggr(out=mv_i[:, 2, :], in_=st_i[2][:])
+        nc.vector.bn_stats(out=st_i[3][:], in_=ig_ps[3][:])
+        centre_i(1)
+        nc.vector.bn_aggr(out=mv_i[:, 3, :], in_=st_i[3][:])
+        std(ln_i, 2, 4, mv_i[:, 2:4, 1])
+        inverse(ln_i, 0, 2)
+        centre_i(2)
+        gates(0)
+        inverse(ln_i, 2, 4)
+        gates(1)
+        nc.vector.tensor_tensor(out=nb[:, 0:2], in0=nmean[:], in1=rs_i[:, 0:2], op=ALU.mult)
+        nc.vector.scalar_tensor_tensor(
+            out=nb[:, 2:4], in0=mv_i[:, 2:4, 0], scalar=-1.0, in1=rs_i[:, 2:4], op0=ALU.mult, op1=ALU.mult
+        )
+        centre_i(3)
+        gates(2)
+        gates(3)
+        for t in range(NT):
+            nc.scalar.activation(
+                out=z_io[t][:], in_=ig_ps[t][:, last], func=ACT.Identity, scale=rs_i[:, t : t + 1], bias=nb[:, t : t + 1]
+            )
+        go_ps = turned_o([z[:] for z in z_io])
 
         halves = (slice(0, 2), slice(2, 4))
         half_tiles = ((0, 1), (2, 3))
-        for hf in halves:
+
+        def forget(hf):
             nc.vector.tensor_tensor(out=m1[:, hf, :], in0=sg[:, hf, AH : 2 * AH], in1=ac_sb[:, hf, :], op=ALU.mult)
+
+        def admit(hf):
             nc.vector.tensor_tensor(out=m2[:, hf, :], in0=sg[:, hf, 0:AH], in1=sg[:, hf, 2 * AH : 3 * AH], op=ALU.mult)
-        for hf in halves:
+
+        def cell(hf):
             nc.vector.tensor_tensor(out=cc[:, hf, :], in0=m1[:, hf, :], in1=m2[:, hf, :], op=ALU.add)
-        mean_var(ln_c, [cc[:, t, :] for t in range(NT)])
-        rstd(ln_c, 0, NT)
-        gate_inputs(slice(3 * AH, 4 * AH), False)
-        nc.scalar.activation(out=sg[:, :, 3 * AH : 4 * AH], in_=gt[:, :, 3 * AH : 4 * AH], func=ACT.Sigmoid)
-        for t in range(NT):
-            centre_gain(a_c[:, t, :], cc[:, t, :], ln_c, t, Wc[:])
+
+        def stats_c(tiles):
+            for t in tiles:
+                nc.vector.bn_stats(out=ln_c[0][t][:], in_=cc[:, t, :])
+
+        def aggr_c(tiles):
+            for t in tiles:
+                nc.vector.bn_aggr(out=ln_c[1][:, t, :], in_=ln_c[0][t][:])
+
+        def centre_c(tiles):
+            for t in tiles:
+                centre_gain(a_c[:, t, :], cc[:, t, :], ln_c, t, Wc[:])
+
+        forget(halves[0])
+        admit(halves[0])
+        cell(halves[0])
+        forget(halves[1])
+        stats_c((0, 1))
+        admit(halves[1])
+        aggr_c((0, 1))
+        cell(halves[1])
+        rstd(ln_c, 0, 2)
+        stats_c((2, 3))
+        nc.vector.scalar_tensor_tensor(
+            out=g_o[:], in0=go_ps[:], scalar=o_gain[:, 1:2], in1=h_o[:], op0=ALU.mult, op1=ALU.add
+        )
+        nc.scalar.activation(out=s_o[:], in_=g_o[:], func=ACT.Sigmoid)
+        aggr_c((2, 3))
+        centre_c((0,))
+        rstd(ln_c, 2, 4)
+        centre_c((1, 2, 3))
+        so_ps = turned_o([s_o[:, t * P : (t + 1) * P] for t in range(NT)])
+        so_v = so_ps[:].rearrange("p (t c) -> p t c", t=NT)
         for hf, tiles in zip(halves, half_tiles):
             for t in tiles:
                 scale_shift(acy[:, t, :], a_c[:, t, :], ln_c, t, Bc[:])
             nc.sync.dma_start(out=o1_v[:, hf, :], in_=acy[:, hf, :])
             nc.scalar.activation(out=th[:, hf, :], in_=acy[:, hf, :], func=ACT.Tanh)
         for hf in halves:
-            nc.vector.tensor_tensor(out=ada[:, hf, :], in0=sg[:, hf, 3 * AH : 4 * AH], in1=th[:, hf, :], op=ALU.mult)
+            nc.vector.tensor_tensor(out=ada[:, hf, :], in0=so_v[:, hf, :], in1=th[:, hf, :], op=ALU.mult)
             nc.sync.dma_start(out=o0_v[:, hf, :], in_=ada[:, hf, :])

@@ -44,10 +44,10 @@ def tile_adaptivelstmcell_pa_kernel(
         nc.vector.memset(eps[:], EPS)
         neghalf = sb.tile([P, NT], F32)
         nc.vector.memset(neghalf[:], -0.5)
-        ident_b = sb.tile([P, P], BF16)
-        make_identity(nc, ident_b[:])
         ident_f = sb.tile([P, P], F32)
         make_identity(nc, ident_f[:])
+        ident_b = sb.tile([P, P], BF16)
+        make_identity(nc, ident_b[:])
 
         def as_row(vec):
             return vec.rearrange("(o n) -> o n", o=1)
@@ -89,7 +89,7 @@ def tile_adaptivelstmcell_pa_kernel(
         whhT = sb.tile([P, N], BF16)
         Wh = sb.tile([P, N], F32)
         Bs = sb.tile([P, N], F32)
-        o_gain = sb.tile([P, 2], F32)
+        o_gain = sb.tile([P, 1], F32)
         o_bias = sb.tile([P, 1], F32)
         z_ho = per_tile([P, AH], F32, "z_ho")
         z_io = per_tile([P, AH], F32, "z_io")
@@ -176,6 +176,10 @@ def tile_adaptivelstmcell_pa_kernel(
                 in_=grouped[:, 4 * c0 : 4 * (c0 + cols)],
             )
 
+        warm_ps = tp.tile([P, 2 * P], F32, tag="tp")
+        for i in range(2):
+            nc.tensor.matmul(warm_ps[:, i * P : (i + 1) * P], lhsT=ident_f[:], rhs=ident_f[:], start=True, stop=True)
+
         ahT_ps = tp.tile([P, NT * P], BF16, tag="tp")
         for t in range(NT):
             nc.tensor.transpose(ahT_ps[:, t * P : (t + 1) * P], ah_sb[:, t * AH : (t + 1) * AH], ident_b[:])
@@ -192,12 +196,25 @@ def tile_adaptivelstmcell_pa_kernel(
                     op0=ALU.subtract, op1=ALU.mult,
                 )
 
+        def centre_h(tiles):
+            for t in tiles:
+                centre_gain(a_h[t][:], hg_ps[t][:, main], ln_h, t, Wh[:, main])
+
+        def quantise_w(j0):
+            for g in range(NG):
+                quantise(w_codes, w_scales, wgrp, g * N + j0 * P, 2 * P)
+
         hg_ps = []
 
         def hidden_product(t):
             hg = acc.tile([P, N], F32, name="hg", tag="acc")
             nc.tensor.matmul(hg[:], lhsT=ahT[:, t * P : (t + 1) * P], rhs=whhT[:], start=True, stop=True)
             hg_ps.append(hg)
+
+        def spread(dst, i):
+            ps = tp.tile([P, N], F32, name="ps_s", tag="tp")
+            nc.tensor.matmul(ps[:], lhsT=ones[:], rhs=rows[:, i * N : (i + 1) * N], start=True, stop=True)
+            nc.scalar.copy(out=dst[:], in_=ps[:])
 
         hidden_product(0)
         hidden_product(1)
@@ -208,20 +225,18 @@ def tile_adaptivelstmcell_pa_kernel(
             if j == 0:
                 hidden_product(2)
                 hidden_product(3)
-                for i, dst in enumerate((Wh, Bs)):
-                    ps = tp.tile([P, N], F32, name="ps_s", tag="tp")
-                    nc.tensor.matmul(ps[:], lhsT=ones[:], rhs=rows[:, i * N : (i + 1) * N], start=True, stop=True)
-                    nc.scalar.copy(out=dst[:], in_=ps[:])
                 mean_var(ln_h, [hg[:] for hg in hg_ps])
+            if j == 1:
                 std(ln_h, 0, NT, ln_h[1][:, :, 1])
-            if j % 2 == 1:
-                for t in (j - 1, j):
-                    centre_gain(a_h[t][:], hg_ps[t][:, main], ln_h, t, Wh[:, main])
-                for g in range(NG):
-                    quantise(w_codes, w_scales, wgrp, g * N + (j - 1) * P, 2 * P)
-                if j == 1:
-                    inverse(ln_h, 0, NT)
-                    norm_ho((0, 1))
+                spread(Wh, 0)
+                quantise_w(0)
+                centre_h((0, 1))
+                inverse(ln_h, 0, NT)
+                norm_ho((0, 1))
+            if j == 2:
+                spread(Bs, 1)
+        centre_h((2, 3))
+        quantise_w(2)
 
         ig_ps = []
         for s in range(NT + 2):
@@ -251,13 +266,12 @@ def tile_adaptivelstmcell_pa_kernel(
                 scale_shift(h_t[t][:], a_h[t][:], ln_h, t, Bs[:, main])
 
         def turned_o(tiles):
-            ps = tp.tile([P, NT * P], F32, name="ps_o", tag="tp")
-            for t in range(NT):
-                nc.tensor.transpose(ps[:, t * P : (t + 1) * P], tiles[t], ident_f[:])
+            ps = tp.tile([P, len(tiles) * P], F32, name="ps_o", tag="tp")
+            for i, tile in enumerate(tiles):
+                nc.tensor.transpose(ps[:, i * P : (i + 1) * P], tile, ident_f[:])
             return ps
 
-        for v in range(2):
-            nc.vector.tensor_copy(out=o_gain[:, v : v + 1], in_=o_raw[v][:, 0:1])
+        nc.vector.tensor_copy(out=o_gain[:], in_=o_raw[0][:, 0:1])
         nc.vector.tensor_tensor(out=o_bias[:], in0=o_raw[2][:, 0:1], in1=o_raw[3][:, 0:1], op=ALU.add)
         ho_ps = turned_o([z[:] for z in z_ho])
 
@@ -269,7 +283,7 @@ def tile_adaptivelstmcell_pa_kernel(
             nc.scalar.activation(
                 out=junk[2 + t][:], in_=ig_ps[t][:], func=ACT.Square, bias=nmean[:, t : t + 1], accum_out=ssd[:, t : t + 1]
             )
-        nc.scalar.activation(out=h_o[:], in_=ho_ps[:], func=ACT.Identity, scale=o_gain[:, 0:1], bias=o_bias[:])
+        nc.scalar.activation(out=h_o[:], in_=ho_ps[:], func=ACT.Identity, scale=o_gain[:], bias=o_bias[:])
 
         def centre_i(t):
             if t < 2:
@@ -345,22 +359,27 @@ def tile_adaptivelstmcell_pa_kernel(
         aggr_c((0, 1))
         cell(halves[1])
         rstd(ln_c, 0, 2)
-        stats_c((2, 3))
-        nc.vector.scalar_tensor_tensor(
-            out=g_o[:], in0=go_ps[:], scalar=o_gain[:, 1:2], in1=h_o[:], op0=ALU.mult, op1=ALU.add
-        )
-        nc.scalar.activation(out=s_o[:], in_=g_o[:], func=ACT.Sigmoid)
-        aggr_c((2, 3))
         centre_c((0,))
-        rstd(ln_c, 2, 4)
-        centre_c((1, 2, 3))
-        so_ps = turned_o([s_o[:, t * P : (t + 1) * P] for t in range(NT)])
-        so_v = so_ps[:].rearrange("p (t c) -> p t c", t=NT)
+        stats_c((2, 3))
+        centre_c((1,))
+        aggr_c((2, 3))
+        so_v = []
+        for tiles in half_tiles:
+            cols = slice(tiles[0] * P, (tiles[1] + 1) * P)
+            nc.vector.scalar_tensor_tensor(
+                out=g_o[:, cols], in0=go_ps[:, cols], scalar=o_raw[1][:, 0:1], in1=h_o[:, cols], op0=ALU.mult, op1=ALU.add
+            )
+            nc.scalar.activation(out=s_o[:, cols], in_=g_o[:, cols], func=ACT.Sigmoid)
+            if tiles == half_tiles[0]:
+                rstd(ln_c, 2, 4)
+            so_ps = turned_o([s_o[:, t * P : (t + 1) * P] for t in tiles])
+            so_v.append(so_ps[:].rearrange("p (t c) -> p t c", t=2))
+        centre_c((2, 3))
         for hf, tiles in zip(halves, half_tiles):
             for t in tiles:
                 scale_shift(acy[:, t, :], a_c[:, t, :], ln_c, t, Bc[:])
             nc.sync.dma_start(out=o1_v[:, hf, :], in_=acy[:, hf, :])
             nc.scalar.activation(out=th[:, hf, :], in_=acy[:, hf, :], func=ACT.Tanh)
-        for hf in halves:
-            nc.vector.tensor_tensor(out=ada[:, hf, :], in0=so_v[:, hf, :], in1=th[:, hf, :], op=ALU.mult)
+        for hf, so in zip(halves, so_v):
+            nc.vector.tensor_tensor(out=ada[:, hf, :], in0=so, in1=th[:, hf, :], op=ALU.mult)
             nc.sync.dma_start(out=o0_v[:, hf, :], in_=ada[:, hf, :])

from contextlib import ExitStack

import concourse.mybir as mybir
from concourse.masks import make_identity

F32 = mybir.dt.float32
BF16 = mybir.dt.bfloat16
U32 = mybir.dt.uint32
U8 = mybir.dt.uint8
FP8X4 = mybir.dt.float8_e4m3fn_x4
ALU = mybir.AluOpType
ACT = mybir.ActivationFunctionType

P = 128
B, I, H, AH, G = 512, 1024, 1024, 128, 4
K = I + H
N = G * AH
NT = B // P
NG = K // 512
EPS = 1e-5
FLOPS = 2 * B * K * N + 2 * B * AH * N


def tile_adaptivelstmcell_pa_kernel(
    tc, x, hx, ah, ac, a_w_ih, a_w_hh, a_ln_i_w, a_ln_i_b, a_ln_h_w, a_ln_h_b, a_ln_c_w, a_ln_c_b, out_0, out_1
):
    nc = tc.nc
    with ExitStack() as ctx:
        sb = ctx.enter_context(tc.tile_pool(name="sb", bufs=1))
        tp = ctx.enter_context(tc.psum_pool(name="tp", bufs=4))
        acc = ctx.enter_context(tc.psum_pool(name="acc", bufs=4))
        ctx.enter_context(tc.manual_schedule())

        def per_tile(shape, dtype, name, align=None):
            return [sb.tile(shape, dtype, name="%s%d" % (name, t), align_bytes=align) for t in range(NT)]

        warm = sb.tile([P, 1], F32)
        nc.vector.memset(warm[:], 0.0)
        rows = sb.tile([P, 2 * N], BF16)
        nc.vector.memset(rows[:].bitcast(F32), 0.0)
        ones = sb.tile([P, P], BF16)
        nc.vector.memset(ones[:], 1.0)
        eps = sb.tile([P, 1], F32)
        nc.vector.memset(eps[:], EPS)
        neghalf = sb.tile([P, NT], F32)
        nc.vector.memset(neghalf[:], -0.5)
        ident_f = sb.tile([P, P], F32)
        make_identity(nc, ident_f[:])
        ident_b = sb.tile([P, P], BF16)
        make_identity(nc, ident_b[:])

        def as_row(vec):
            return vec.rearrange("(o n) -> o n", o=1)

        ah_sb = sb.tile([P, NT * AH], BF16)
        nc.sync.dma_start(out=ah_sb[:], in_=ah.rearrange("(p t) k -> p (t k)", t=NT))
        whh_sb = sb.tile([P, G, AH], BF16)
        nc.sync.dma_start(out=whh_sb[:], in_=a_w_hh.rearrange("(j p) k -> p j k", p=P))
        warm2 = sb.tile([P, 1], F32)
        nc.scalar.activation(out=warm2[:], in_=warm[:], func=ACT.Sqrt)
        nc.scalar.dma_start(out=rows[0:1, 0:N], in_=as_row(a_ln_h_w))
        nc.scalar.dma_start(out=rows[0:1, N : 2 * N], in_=as_row(a_ln_i_b))
        nc.scalar.dma_start(out=rows[1:2, N : 2 * N], in_=as_row(a_ln_h_b))
        w_sb = per_tile([P, K], BF16, "w_sb")
        for j in range(G):
            nc.sync.dma_start(out=w_sb[j][:], in_=a_w_ih[j * P : (j + 1) * P, :])
        a_sb = per_tile([P, K], BF16, "a_sb")
        x_v = x.rearrange("(p t) k -> p t k", t=NT)
        hx_v = hx.rearrange("(p t) k -> p t k", t=NT)
        for t in range(NT):
            nc.sync.dma_start(out=a_sb[t][:, 0:I], in_=x_v[:, t, :])
            nc.sync.dma_start(out=a_sb[t][:, I:K], in_=hx_v[:, t, :])
        ac_sb = sb.tile([P, NT, AH], BF16)
        nc.sync.dma_start(out=ac_sb[:], in_=ac.rearrange("(p t) c -> p t c", t=NT))
        main, last = slice(0, 3 * AH), slice(3 * AH, N)
        Wi = sb.tile([P, 3 * AH], BF16)
        nc.sync.dma_start(out=Wi[:], in_=a_ln_i_w[main].partition_broadcast(P))
        Wc = sb.tile([P, AH], BF16)
        nc.sync.dma_start(out=Wc[:], in_=a_ln_c_w.partition_broadcast(P))
        Bc = sb.tile([P, AH], BF16)
        nc.sync.dma_start(out=Bc[:], in_=a_ln_c_b.partition_broadcast(P))
        o_raw = []
        for v, vec in enumerate((a_ln_h_w, a_ln_i_w, a_ln_i_b, a_ln_h_b)):
            col = sb.tile([P, 2], BF16, name="o_raw%d" % v)
            nc.sync.dma_start(out=col[:, 0:1], in_=vec[last].rearrange("(p o) -> p o", o=1))
            o_raw.append(col)

        ahT = sb.tile([P, NT * P], BF16)
        whhT = sb.tile([P, N], BF16)
        Wh = sb.tile([P, N], F32)
        Bs = sb.tile([P, N], F32)
        o_gain = sb.tile([P, 1], F32)
        o_bias = sb.tile([P, 1], F32)
        z_ho = per_tile([P, AH], F32, "z_ho")
        z_io = per_tile([P, AH], F32, "z_io")
        h_o = sb.tile([P, NT * P], F32)
        g_o = sb.tile([P, NT * P], F32)
        s_o = sb.tile([P, NT * P], F32)
        junk = per_tile([P, N], F32, "junk")
        nmean = sb.tile([P, 2], F32)
        ssd = sb.tile([P, 2], F32)
        nb = sb.tile([P, NT], F32)
        wgrp = sb.tile([P, NG * N * 4], BF16, align_bytes=64)
        wgrp_f = wgrp[:].bitcast(F32).rearrange("p (g j r u) -> p g j r u", g=NG, j=G, u=2)
        w_codes = sb.tile([P, NG * N], U32, align_bytes=64)
        w_scales = sb.tile([P, NG * N], U8, align_bytes=64)
        agrp = per_tile([P, NG * P * 4], BF16, "agrp", 64)
        a_codes = per_tile([P, NG * P], U32, "a_codes", 64)
        a_scales = per_tile([P, NG * P], U8, "a_scales", 64)
        a_h = per_tile([P, 3 * AH], F32, "a_h")
        h_t = per_tile([P, 3 * AH], F32, "h_t")
        a_i = per_tile([P, 3 * AH], F32, "a_i")
        gt = sb.tile([P, NT, 3 * AH], F32)
        sg = sb.tile([P, NT, 3 * AH], F32)
        m1 = sb.tile([P, NT, AH], F32)
        m2 = sb.tile([P, NT, AH], F32)
        cc = sb.tile([P, NT, AH], F32)
        a_c = sb.tile([P, NT, AH], F32)
        acy = sb.tile([P, NT, AH], F32)
        th = sb.tile([P, NT, AH], F32)
        ada = sb.tile([P, NT, AH], F32)
        o0_v = out_0.rearrange("(p t) c -> p t c", t=NT)
        o1_v = out_1.rearrange("(p t) c -> p t c", t=NT)

        def norm_tiles(name):
            st = per_tile([P, 6], F32, "st_" + name)
            mv = sb.tile([P, NT, 2], F32, name="mv_" + name)
            ve = sb.tile([P, NT], F32, name="ve_" + name)
            rs = sb.tile([P, NT], F32, name="rs_" + name)
            return st, mv, ve, rs

        def mean_var(tiles, srcs):
            st, mv, ve, rs = tiles
            for t in range(NT):
                nc.vector.bn_stats(out=st[t][:], in_=srcs[t])
            for t in range(NT):
                nc.vector.bn_aggr(out=mv[:, t, :], in_=st[t][:])

        def rstd(tiles, t0, t1):
            st, mv, ve, rs = tiles
            nc.vector.tensor_scalar_add(out=ve[:, t0:t1], in0=mv[:, t0:t1, 1], scalar1=EPS)
            nc.gpsimd.tensor_tensor(out=rs[:, t0:t1], in0=ve[:, t0:t1], in1=neghalf[:, t0:t1], op=ALU.pow)

        def std(tiles, t0, t1, var, scale=1.0):
            nc.scalar.activation(out=tiles[2][:, t0:t1], in_=var, func=ACT.Sqrt, scale=scale, bias=eps[:])

        def inverse(tiles, t0, t1):
            nc.vector.reciprocal(out=tiles[3][:, t0:t1], in_=tiles[2][:, t0:t1])

        def centre_gain(out, src, tiles, t, gain):
            nc.vector.scalar_tensor_tensor(
                out=out, in0=src, scalar=tiles[1][:, t, 0:1], in1=gain, op0=ALU.subtract, op1=ALU.mult
            )

        def scale_shift(out, src, tiles, t, shift):
            nc.vector.scalar_tensor_tensor(
                out=out, in0=src, scalar=tiles[3][:, t : t + 1], in1=shift, op0=ALU.mult, op1=ALU.add
            )

        ln_h = norm_tiles("h")
        ln_i = norm_tiles("i")
        ln_c = norm_tiles("c")

        def transposed_bank(src, h):
            src_f = src[:].bitcast(F32)
            ps = tp.tile([P, 4 * P], F32, name="ps_t", tag="tp")
            for i in range(4):
                c0 = 512 * h + P * i
                nc.tensor.transpose(ps[:, i * P : (i + 1) * P], src_f[:, c0 : c0 + P], ident_f[:])
            return ps[:].rearrange("p (g u r) -> p g r u", g=2, u=2)

        def quantise(codes, scales, grouped, c0, cols):
            nc.vector.quantize_mx(
                out=codes[:, c0 : c0 + cols].bitcast(FP8X4),
                scales=scales[:, c0 : c0 + cols],
                in_=grouped[:, 4 * c0 : 4 * (c0 + cols)],
            )

        warm_ps = tp.tile([P, 2 * P], F32, tag="tp")
        for i in range(2):
            nc.tensor.matmul(warm_ps[:, i * P : (i + 1) * P], lhsT=ident_f[:], rhs=ident_f[:], start=True, stop=True)

        ahT_ps = tp.tile([P, NT * P], BF16, tag="tp")
        for t in range(NT):
            nc.tensor.transpose(ahT_ps[:, t * P : (t + 1) * P], ah_sb[:, t * AH : (t + 1) * AH], ident_b[:])
        whhT_ps = tp.tile([P, N], BF16, tag="tp")
        for j in range(G):
            nc.tensor.transpose(whhT_ps[:, j * P : (j + 1) * P], whh_sb[:, j, :], ident_b[:])
        nc.vector.tensor_copy(out=ahT[:], in_=ahT_ps[:])
        nc.vector.tensor_copy(out=whhT[:], in_=whhT_ps[:])

        def norm_ho(tiles):
            for t in tiles:
                nc.vector.tensor_scalar(
                    out=z_ho[t][:], in0=hg_ps[t][:, last], scalar1=ln_h[1][:, t, 0:1], scalar2=ln_h[3][:, t : t + 1],
                    op0=ALU.subtract, op1=ALU.mult,
                )

        def centre_h(tiles):
            for t in tiles:
                centre_gain(a_h[t][:], hg_ps[t][:, main], ln_h, t, Wh[:, main])

        def quantise_w(j0):
            for g in range(NG):
                quantise(w_codes, w_scales, wgrp, g * N + j0 * P, 2 * P)

        hg_ps = []

        def hidden_product(t):
            hg = acc.tile([P, N], F32, name="hg", tag="acc")
            nc.tensor.matmul(hg[:], lhsT=ahT[:, t * P : (t + 1) * P], rhs=whhT[:], start=True, stop=True)
            hg_ps.append(hg)

        def spread(dst, i):
            ps = tp.tile([P, N], F32, name="ps_s", tag="tp")
            nc.tensor.matmul(ps[:], lhsT=ones[:], rhs=rows[:, i * N : (i + 1) * N], start=True, stop=True)
            nc.scalar.copy(out=dst[:], in_=ps[:])

        hidden_product(0)
        hidden_product(1)
        for j in range(G):
            banks = [transposed_bank(w_sb[j], h) for h in range(2)]
            for h in range(2):
                nc.scalar.copy(out=wgrp_f[:, 2 * h : 2 * h + 2, j, :, :], in_=banks[h])
            if j == 0:
                hidden_product(2)
                hidden_product(3)
                mean_var(ln_h, [hg[:] for hg in hg_ps])
            if j == 1:
                std(ln_h, 0, NT, ln_h[1][:, :, 1])
                spread(Wh, 0)
                quantise_w(0)
                centre_h((0, 1))
                inverse(ln_h, 0, NT)
                norm_ho((0, 1))
            if j == 2:
                spread(Bs, 1)
        centre_h((2, 3))
        quantise_w(2)

        ig_ps = []
        for s in range(NT + 2):
            if s < NT:
                banks = [transposed_bank(a_sb[s], h) for h in range(2)]
                agrp_f = agrp[s][:].bitcast(F32).rearrange("p (g r u) -> p g r u", g=NG, u=2)
                for h in range(2):
                    nc.scalar.copy(out=agrp_f[:, 2 * h : 2 * h + 2, :, :], in_=banks[h])
            if s >= 2:
                t = s - 2
                for h in range(2):
                    quantise(a_codes[t], a_scales[t], agrp[t], h * 2 * P, 2 * P)
                ig = acc.tile([P, N], F32, name="ig", tag="acc")
                for g in range(NG):
                    nc.tensor.matmul_mx(
                        out=ig[:],
                        lhsT=a_codes[t][:, g * P : (g + 1) * P].bitcast(FP8X4),
                        lhsT_scale=a_scales[t][:, g * P : (g + 1) * P],
                        rhs=w_codes[:, g * N : (g + 1) * N].bitcast(FP8X4),
                        rhs_scale=w_scales[:, g * N : (g + 1) * N],
                        start=(g == 0),
                        stop=(g == NG - 1),
                    )
                ig_ps.append(ig)
                if t == 0:
                    norm_ho((2, 3))
                scale_shift(h_t[t][:], a_h[t][:], ln_h, t, Bs[:, main])

        def turned_o(tiles):
            ps = tp.tile([P, len(tiles) * P], F32, name="ps_o", tag="tp")
            for i, tile in enumerate(tiles):
                nc.tensor.transpose(ps[:, i * P : (i + 1) * P], tile, ident_f[:])
            return ps

        nc.vector.tensor_copy(out=o_gain[:], in_=o_raw[0][:, 0:1])
        nc.vector.tensor_tensor(out=o_bias[:], in0=o_raw[2][:, 0:1], in1=o_raw[3][:, 0:1], op=ALU.add)
        ho_ps = turned_o([z[:] for z in z_ho])

        for t in range(2):
            nc.scalar.activation(
                out=junk[t][:], in_=ig_ps[t][:], func=ACT.Identity, scale=-1.0 / N, accum_out=nmean[:, t : t + 1]
            )
        for t in range(2):
            nc.scalar.activation(
                out=junk[2 + t][:], in_=ig_ps[t][:], func=ACT.Square, bias=nmean[:, t : t + 1], accum_out=ssd[:, t : t + 1]
            )
        nc.scalar.activation(out=h_o[:], in_=ho_ps[:], func=ACT.Identity, scale=o_gain[:], bias=o_bias[:])

        def centre_i(t):
            if t < 2:
                nc.vector.scalar_tensor_tensor(
                    out=a_i[t][:], in0=ig_ps[t][:, main], scalar=nmean[:, t : t + 1], in1=Wi[:], op0=ALU.add, op1=ALU.mult
                )
            else:
                centre_gain(a_i[t][:], ig_ps[t][:, main], ln_i, t, Wi[:])

        st_i, mv_i, ve_i, rs_i = ln_i

        def gates(t):
            scale_shift(gt[:, t, :], a_i[t][:], ln_i, t, h_t[t][:])
            nc.scalar.activation(out=sg[:, t, 0 : 2 * AH], in_=gt[:, t, 0 : 2 * AH], func=ACT.Sigmoid)
            nc.scalar.activation(out=sg[:, t, 2 * AH : 3 * AH], in_=gt[:, t, 2 * AH : 3 * AH], func=ACT.Tanh)

        std(ln_i, 0, 2, ssd[:], 1.0 / N)
        nc.vector.bn_stats(out=st_i[2][:], in_=ig_ps[2][:])
        centre_i(0)
        nc.vector.bn_aggr(out=mv_i[:, 2, :], in_=st_i[2][:])
        nc.vector.bn_stats(out=st_i[3][:], in_=ig_ps[3][:])
        centre_i(1)
        nc.vector.bn_aggr(out=mv_i[:, 3, :], in_=st_i[3][:])
        std(ln_i, 2, 4, mv_i[:, 2:4, 1])
        inverse(ln_i, 0, 2)
        centre_i(2)
        gates(0)
        inverse(ln_i, 2, 4)
        gates(1)
        nc.vector.tensor_tensor(out=nb[:, 0:2], in0=nmean[:], in1=rs_i[:, 0:2], op=ALU.mult)
        nc.vector.scalar_tensor_tensor(
            out=nb[:, 2:4], in0=mv_i[:, 2:4, 0], scalar=-1.0, in1=rs_i[:, 2:4], op0=ALU.mult, op1=ALU.mult
        )
        centre_i(3)
        gates(2)
        gates(3)
        for t in range(NT):
            nc.scalar.activation(
                out=z_io[t][:], in_=ig_ps[t][:, last], func=ACT.Identity, scale=rs_i[:, t : t + 1], bias=nb[:, t : t + 1]
            )
        go_ps = turned_o([z[:] for z in z_io])

        halves = (slice(0, 2), slice(2, 4))
        half_tiles = ((0, 1), (2, 3))

        def forget(hf):
            nc.vector.tensor_tensor(out=m1[:, hf, :], in0=sg[:, hf, AH : 2 * AH], in1=ac_sb[:, hf, :], op=ALU.mult)

        def admit(hf):
            nc.vector.tensor_tensor(out=m2[:, hf, :], in0=sg[:, hf, 0:AH], in1=sg[:, hf, 2 * AH : 3 * AH], op=ALU.mult)

        def cell(hf):
            nc.vector.tensor_tensor(out=cc[:, hf, :], in0=m1[:, hf, :], in1=m2[:, hf, :], op=ALU.add)

        def stats_c(tiles):
            for t in tiles:
                nc.vector.bn_stats(out=ln_c[0][t][:], in_=cc[:, t, :])

        def aggr_c(tiles):
            for t in tiles:
                nc.vector.bn_aggr(out=ln_c[1][:, t, :], in_=ln_c[0][t][:])

        def centre_c(tiles):
            for t in tiles:
                centre_gain(a_c[:, t, :], cc[:, t, :], ln_c, t, Wc[:])

        forget(halves[0])
        admit(halves[0])
        cell(halves[0])
        forget(halves[1])
        stats_c((0, 1))
        admit(halves[1])
        aggr_c((0, 1))
        cell(halves[1])
        rstd(ln_c, 0, 2)
        centre_c((0,))
        stats_c((2, 3))
        centre_c((1,))
        aggr_c((2, 3))
        so_v = []
        for tiles in half_tiles:
            cols = slice(tiles[0] * P, (tiles[1] + 1) * P)
            nc.vector.scalar_tensor_tensor(
                out=g_o[:, cols], in0=go_ps[:, cols], scalar=o_raw[1][:, 0:1], in1=h_o[:, cols], op0=ALU.mult, op1=ALU.add
            )
            nc.scalar.activation(out=s_o[:, cols], in_=g_o[:, cols], func=ACT.Sigmoid)
            if tiles == half_tiles[0]:
                rstd(ln_c, 2, 4)
            so_ps = turned_o([s_o[:, t * P : (t + 1) * P] for t in tiles])
            so_v.append(so_ps[:].rearrange("p (t c) -> p t c", t=2))
        centre_c((2, 3))
        for hf, tiles in zip(halves, half_tiles):
            for t in tiles:
                scale_shift(acy[:, t, :], a_c[:, t, :], ln_c, t, Bc[:])
            nc.sync.dma_start(out=o1_v[:, hf, :], in_=acy[:, hf, :])
            nc.scalar.activation(out=th[:, hf, :], in_=acy[:, hf, :], func=ACT.Tanh)
        for hf, so in zip(halves, so_v):
            nc.vector.tensor_tensor(out=ada[:, hf, :], in0=so, in1=th[:, hf, :], op=ALU.mult)
            nc.sync.dma_start(out=o0_v[:, hf, :], in_=ada[:, hf, :])
